import numpy as np
import ml_dtypes


def mxq(x, axis, fmt="e4m3"):
    dtype, down = {"e4m3": (ml_dtypes.float8_e4m3fn, 7), "e5m2": (ml_dtypes.float8_e5m2, 14)}[fmt]
    v = np.moveaxis(np.asarray(x, np.float32).astype(ml_dtypes.bfloat16).astype(np.float64), axis, -1)
    blocks = v.reshape(v.shape[:-1] + (-1, 32))
    amax = np.abs(blocks).max(-1, keepdims=True)
    byte = np.maximum(np.where(amax > 0, np.frexp(amax)[1] - 1 + 127, 0) - down, 1)
    scale = np.exp2(byte - 127.0)
    codes = (blocks / scale).astype(np.float32).astype(dtype).astype(np.float64)
    return np.moveaxis((codes * scale).reshape(v.shape), -1, axis)


WIDE = False


def mx_kscale(k):
    if not WIDE:
        return np.ones(k)
    levels = np.array([10, -10, 5, -5, 0])
    a = np.random.permutation(np.resize(levels, k // 512 * 4)).reshape(k // 512, 4)
    idx = np.arange(k)
    return np.exp2(a[idx // 512, idx % 128 // 32])


BF16 = ml_dtypes.bfloat16


def bf(x):
    return np.asarray(x, np.float32).astype(BF16)


def f64(x):
    return np.asarray(x).astype(np.float64)


B, T, D, NH, HD, QB = 1, 1024, 1024, 8, 256, 512
H2 = NH // 2
HD2 = HD // 2
MXB = 32
LAMBDA_INIT = 0.8 - 0.6 * np.exp(-0.3 * 0)


def setup_inputs():
    m = np.sqrt(0.3 / HD2)
    s = f64(mx_kscale(T))
    s[:MXB] = s.max()
    q = np.random.standard_normal((B, T, NH, HD))
    k = np.random.standard_normal((B, T, NH, HD))
    q[..., 0] = np.sqrt(HD)
    k[..., 0] += np.log(s)[None, :, None]
    v = np.random.standard_normal((B, T, H2, 2 * HD)) * 2.0 * (s.max() / s)[None, :, None, None]
    return {"q_rot": bf(q),
            "k_rot": bf(k),
            "v": bf(v),
            "lambda_q1": bf(np.random.standard_normal(HD2) * 0.1 + m),
            "lambda_k1": bf(np.random.standard_normal(HD2) * 0.1 + m),
            "lambda_q2": bf(np.random.standard_normal(HD2) * 0.1 + m),
            "lambda_k2": bf(np.random.standard_normal(HD2) * 0.1 - m)}


def causal_attention(q, k, vq):
    rows = []
    for i in range(T // QB):
        lo, hi = i * QB, (i + 1) * QB
        s = q[:, :, lo:hi] @ k[:, :, :hi].transpose(0, 1, 3, 2) * (1.0 / np.sqrt(HD))
        keep = np.arange(hi)[None, :] <= np.arange(lo, hi)[:, None]
        s = np.where(keep, s, -np.inf)
        e = np.exp(s - s.max(-1, keepdims=True))
        rows.append((mxq(e, 3, "e4m3") @ vq[:, :, :hi]) / e.sum(-1, keepdims=True))
    return np.concatenate(rows, axis=2).transpose(0, 2, 1, 3)


def reference(q_rot, k_rot, v, lambda_q1, lambda_k1, lambda_q2, lambda_k2):
    q = f64(q_rot).reshape(B, T, 2, H2, HD).transpose(2, 0, 3, 1, 4)
    k = f64(k_rot).reshape(B, T, 2, H2, HD).transpose(2, 0, 3, 1, 4)
    vq = mxq(f64(v).transpose(0, 2, 1, 3), 2, "e4m3")
    y1 = causal_attention(q[0], k[0], vq)
    y2 = causal_attention(q[1], k[1], vq)
    lam1 = np.exp(np.sum(f64(lambda_q1) * f64(lambda_k1)))
    lam2 = np.exp(np.sum(f64(lambda_q2) * f64(lambda_k2)))
    lam = lam1 - lam2 + LAMBDA_INIT
    return (y1 - lam * y2).reshape(B, T, NH * HD)

@@ -1,0 +1,333 @@
+import math
+from contextlib import ExitStack
+
+import concourse.mybir as mybir
+from concourse.masks import make_identity
+
+F32 = mybir.dt.float32
+BF16 = mybir.dt.bfloat16
+U32 = mybir.dt.uint32
+U8 = mybir.dt.uint8
+FP8X4 = mybir.dt.float8_e4m3fn_x4
+ALU = mybir.AluOpType
+ACT = mybir.ActivationFunctionType
+AXIS = mybir.AxisListType
+
+P = 128
+PACK = 4
+K_PASS = P * PACK
+SEQ = 1024
+N_TILES = SEQ // P
+TILES_PER_PASS = K_PASS // P
+RUN = P // PACK
+N_HEADS = 8
+N_GROUPS = 2
+N_VHEADS = 4
+HEAD_DIM = 256
+V_WIDTH = 512
+SCALE = 1.0 / math.sqrt(HEAD_DIM)
+LAMBDA_INIT = 0.8 - 0.6 * math.exp(-0.3 * 0)
+MASKED = -1.0e30
+N_UNITS = N_TILES * N_VHEADS
+
+FLOPS = N_HEADS * (512 * 512 + 512 * 1024) * 2 * (HEAD_DIM + V_WIDTH)
+
+
+def tile_mixerdiffattention_pb_kernel(
+    tc, q_rot, k_rot, v, lambda_q1, lambda_k1, lambda_q2, lambda_k2, out
+):
+    nc = tc.nc
+    with ExitStack() as ctx:
+        keep = ctx.enter_context(tc.tile_pool(name="keep", bufs=1))
+        raw = ctx.enter_context(tc.tile_pool(name="raw", bufs=4))
+        work = ctx.enter_context(tc.tile_pool(name="work", bufs=3))
+        small = ctx.enter_context(tc.tile_pool(name="small", bufs=6))
+        psum_s = ctx.enter_context(tc.psum_pool(name="psum_s", bufs=4))
+        psum_t = ctx.enter_context(tc.psum_pool(name="psum_t", bufs=2))
+        psum_y = ctx.enter_context(tc.psum_pool(name="psum_y", bufs=2))
+
+        q_tiles = q_rot[0].rearrange("(i p) h d -> i p (h d)", p=P)
+        k_tiles = k_rot[0].rearrange("(i p) h d -> i p (h d)", p=P)
+        v_rows = v[0].rearrange("(g p j) h c -> g h p j c", p=P, j=PACK)
+        out_tiles = out[0].rearrange("(i p) f -> i p f", p=P)
+
+        q_raw = {}
+        k_raw = {}
+        v_raw = {}
+
+        def load_q_and_k(i):
+            q_raw[i] = raw.tile([P, N_HEADS * HEAD_DIM], BF16, name="q_raw")
+            nc.sync.dma_start(out=q_raw[i][:], in_=q_tiles[i])
+            k_raw[i] = raw.tile([P, N_HEADS * HEAD_DIM], BF16, name="k_raw")
+            nc.sync.dma_start(out=k_raw[i][:], in_=k_tiles[i])
+
+        def load_v(g, h):
+            v_raw[g, h] = raw.tile([P, PACK, V_WIDTH], BF16, name="v_raw")
+            nc.sync.dma_start(out=v_raw[g, h][:], in_=v_rows[g, h])
+
+        load_q_and_k(0)
+        for h in range(N_VHEADS):
+            load_v(0, h)
+        for i in range(1, 4):
+            load_q_and_k(i)
+
+        ident_f32 = keep.tile([P, P], F32, name="ident_f32")
+        make_identity(nc, ident_f32[:])
+        ident_bf16 = keep.tile([P, P], BF16, name="ident_bf16")
+        make_identity(nc, ident_bf16[:])
+        to_planes = keep.tile([P, P], F32, name="to_planes")
+        nc.vector.tensor_copy(
+            out=to_planes[:].rearrange("p (t r) -> p t r", t=PACK),
+            in_=ident_f32[:].rearrange("p (r t) -> p t r", t=PACK),
+        )
+        mask_f32 = keep.tile([P, P], F32, name="mask_f32")
+        nc.gpsimd.memset(mask_f32[:], 0.0)
+        nc.gpsimd.affine_select(
+            out=mask_f32[:],
+            in_=mask_f32[:],
+            compare_op=ALU.is_ge,
+            fill=MASKED,
+            base=0,
+            pattern=[[-1, P]],
+            channel_multiplier=1,
+        )
+        mask = keep.tile([P, PACK, RUN], BF16, name="mask")
+        nc.vector.tensor_copy(
+            out=mask[:], in_=mask_f32[:].rearrange("p (r t) -> p t r", t=PACK)
+        )
+
+        lam_in = keep.tile([P, 4, P], BF16, name="lam_in")
+        for n, vec in enumerate((lambda_q1, lambda_q2, lambda_k1, lambda_k2)):
+            nc.scalar.dma_start(out=lam_in[:, n, :], in_=vec.partition_broadcast(P))
+        lam_prod = keep.tile([P, N_GROUPS, P], F32, name="lam_prod")
+        nc.vector.tensor_tensor(
+            out=lam_prod[:], in0=lam_in[:, 0:2, :], in1=lam_in[:, 2:4, :], op=ALU.mult
+        )
+        lam_dot = keep.tile([P, N_GROUPS], F32, name="lam_dot")
+        nc.vector.tensor_reduce(out=lam_dot[:], in_=lam_prod[:], axis=AXIS.X, op=ALU.add)
+        lam_exp = keep.tile([P, N_GROUPS], F32, name="lam_exp")
+        nc.scalar.activation(out=lam_exp[:], in_=lam_dot[:], func=ACT.Exp)
+        weights = keep.tile([P, N_GROUPS], F32, name="weights")
+        nc.vector.memset(weights[:, 0:1], 1.0)
+        nc.vector.tensor_scalar(
+            out=weights[:, 1:2],
+            in0=lam_exp[:, 1:2],
+            scalar1=lam_exp[:, 0:1],
+            scalar2=LAMBDA_INIT,
+            op0=ALU.subtract,
+            op1=ALU.subtract,
+        )
+
+        e_bufs = []
+        for n in range(2 * N_GROUPS):
+            e_buf = keep.tile([P, 2, PACK, P], BF16, name="e_buf%d" % n)
+            nc.vector.memset(e_buf[:], 0.0)
+            e_bufs.append(e_buf)
+
+        q_t = keep.tile([P, N_TILES, N_HEADS, P], F32, name="q_t")
+        k_t = keep.tile([P, N_HEADS, SEQ], F32, name="k_t")
+        q_pairs = q_t[:].bitcast(BF16).rearrange("w i h (q e) -> w i h q e", e=2)
+        k_pairs = k_t[:].bitcast(BF16).rearrange(
+            "w h (g t p e) -> w h g t p e", t=PACK, p=P, e=2
+        )
+        k_words = k_t[:].rearrange("w h (g t p) -> w h g t p", t=PACK, p=P)
+
+        def transpose_q_and_k(i, half):
+            heads = slice(4 * half, 4 * half + 4)
+            g, column = i // TILES_PER_PASS, RUN * (i % TILES_PER_PASS)
+            q_bank = psum_s.tile([P, 4, P], F32, tag="s", name="q_bank")
+            k_bank = psum_s.tile([P, 4, P], F32, tag="s", name="k_bank")
+            for a in range(4):
+                words = slice((4 * half + a) * P, (4 * half + a + 1) * P)
+                nc.tensor.transpose(q_bank[:, a, :], q_raw[i][:].bitcast(F32)[:, words], ident_f32[:])
+            for a in range(4):
+                words = slice((4 * half + a) * P, (4 * half + a + 1) * P)
+                nc.tensor.transpose(k_bank[:, a, :], k_raw[i][:].bitcast(F32)[:, words], to_planes[:])
+            nc.scalar.copy(out=q_t[:, i, heads, :], in_=q_bank[:])
+            nc.vector.tensor_copy(
+                out=k_words[:, heads, g, :, column : column + RUN],
+                in_=k_bank[:].rearrange("w a (t r) -> w a t r", t=PACK),
+            )
+
+        v_codes = keep.tile([P, 2, N_VHEADS, V_WIDTH], U32, name="v_codes", align_bytes=64)
+        v_scales = keep.tile([P, 2, N_VHEADS, V_WIDTH], U8, name="v_scales", align_bytes=64)
+
+        def quantise_v(g, h):
+            v_grouped = work.tile([P, V_WIDTH, PACK], BF16, name="v_grouped", align_bytes=64)
+            nc.vector.tensor_copy(
+                out=v_grouped[:].rearrange("p (c n) j -> p c j n", n=4),
+                in_=v_raw[g, h][:].rearrange("p j (c n) -> p c j n", n=4),
+            )
+            nc.vector.quantize_mx(
+                out=v_codes[:, g, h, :].bitcast(FP8X4),
+                scales=v_scales[:, g, h, :],
+                in_=v_grouped[:].rearrange("p c j -> p (c j)"),
+            )
+
+        sums = {}
+        planes = {}
+        e_grouped = {}
+        e_codes = {}
+        e_scales = {}
+
+        def passes_of(unit):
+            return (unit // N_VHEADS) // TILES_PER_PASS + 1
+
+        def scores_and_exp(unit):
+            i, h = unit // N_VHEADS, unit % N_VHEADS
+            n_pass = passes_of(unit)
+            sums[unit] = small.tile([P, N_GROUPS, n_pass], F32, name="sums")
+            for grp in range(N_GROUPS):
+                head = N_VHEADS * grp + h
+                e_buf = e_bufs[N_GROUPS * (unit % 2) + grp]
+                banks = []
+                widths = []
+                for g in range(n_pass):
+                    last = g == n_pass - 1
+                    width = RUN * (i % TILES_PER_PASS + 1) if last else P
+                    s = psum_s.tile([P, PACK, P], F32, tag="s", name="s")
+                    for parity in range(2):
+                        nc.tensor.matmul(
+                            out=s[:, :, 0:width],
+                            lhsT=q_pairs[:, i, head, :, parity],
+                            rhs=k_pairs[:, head, g, :, 0:width, parity],
+                            start=(parity == 0),
+                            stop=(parity == 1 and not last),
+                        )
+                    if last:
+                        nc.tensor.matmul(
+                            out=s[:, :, width - RUN : width],
+                            lhsT=ident_bf16[:],
+                            rhs=mask[:],
+                            start=False,
+                            stop=True,
+                        )
+                    banks.append(s)
+                    widths.append(width)
+                top = small.tile([P, n_pass], F32, name="top")
+                for g in range(n_pass):
+                    nc.vector.tensor_reduce(
+                        out=top[:, g : g + 1],
+                        in_=banks[g][:, :, 0 : widths[g]],
+                        axis=AXIS.XY,
+                        op=ALU.max,
+                    )
+                shift = small.tile([P, 1], F32, name="shift")
+                if n_pass == 1:
+                    nc.vector.tensor_scalar(
+                        out=shift[:], in0=top[:, 0:1], scalar1=-SCALE, scalar2=None, op0=ALU.mult
+                    )
+                else:
+                    nc.vector.tensor_scalar(
+                        out=shift[:],
+                        in0=top[:, 0:1],
+                        scalar1=top[:, 1:2],
+                        scalar2=-SCALE,
+                        op0=ALU.max,
+                        op1=ALU.mult,
+                    )
+                for g in range(n_pass):
+                    nc.scalar.activation(
+                        out=e_buf[:, g, :, 0 : widths[g]],
+                        in_=banks[g][:, :, 0 : widths[g]],
+                        func=ACT.Exp,
+                        bias=shift[:, 0:1],
+                        scale=SCALE,
+                        accum_out=sums[unit][:, grp, g : g + 1],
+                    )
+
+        def transpose_e(unit):
+            h = unit % N_VHEADS
+            n_pass = passes_of(unit)
+            e_grouped[unit] = work.tile(
+                [P, N_GROUPS, n_pass, P, PACK], BF16, name="e_grouped", align_bytes=64
+            )
+            for grp in range(N_GROUPS):
+                e_buf = e_bufs[N_GROUPS * (unit % 2) + grp]
+                planes[grp] = psum_t.tile([P, n_pass, PACK, P], BF16, tag="t", name="planes")
+                for g in range(n_pass):
+                    for t in range(PACK):
+                        nc.tensor.transpose(planes[grp][:, g, t, :], e_buf[:, g, t, :], ident_bf16[:])
+            for grp in range(N_GROUPS):
+                source = planes[grp][:].rearrange("p g t q -> p g q t")
+                if grp == 1 and h % 2 == 1:
+                    nc.vector.tensor_copy(out=e_grouped[unit][:, grp], in_=source)
+                else:
+                    nc.scalar.copy(out=e_grouped[unit][:, grp], in_=source)
+
+        def quantise_e(unit):
+            n_pass = passes_of(unit)
+            width = N_GROUPS * n_pass * P
+            e_codes[unit] = work.tile([P, width], U32, name="e_codes", align_bytes=64)
+            e_scales[unit] = work.tile([P, width], U8, name="e_scales", align_bytes=64)
+            nc.vector.quantize_mx(
+                out=e_codes[unit][:].bitcast(FP8X4),
+                scales=e_scales[unit][:],
+                in_=e_grouped[unit][:].rearrange("p a g q t -> p (a g q t)"),
+            )
+
+        def attend_and_combine(unit):
+            i, h = unit // N_VHEADS, unit % N_VHEADS
+            n_pass = passes_of(unit)
+            y = []
+            for grp in range(N_GROUPS):
+                acc = psum_y.tile([P, V_WIDTH], F32, tag="y", name="acc")
+                for g in range(n_pass):
+                    cols = slice((grp * n_pass + g) * P, (grp * n_pass + g + 1) * P)
+                    nc.tensor.matmul_mx(
+                        out=acc[:],
+                        lhsT=e_codes[unit][:, cols].bitcast(FP8X4),
+                        lhsT_scale=e_scales[unit][:, cols],
+                        rhs=v_codes[:, g, h, :].bitcast(FP8X4),
+                        rhs_scale=v_scales[:, g, h, :],
+                        start=(g == 0),
+                        stop=(g == n_pass - 1),
+                    )
+                y.append(acc)
+            inverse = small.tile([P, N_GROUPS], F32, name="inverse")
+            if n_pass == 1:
+                nc.vector.reciprocal(out=inverse[:], in_=sums[unit][:, :, 0])
+            else:
+                total = small.tile([P, N_GROUPS], F32, name="total")
+                nc.vector.tensor_reduce(out=total[:], in_=sums[unit][:], axis=AXIS.X, op=ALU.add)
+                nc.vector.reciprocal(out=inverse[:], in_=total[:])
+            factor = small.tile([P, N_GROUPS], F32, name="factor")
+            nc.vector.tensor_tensor(out=factor[:], in0=inverse[:], in1=weights[:], op=ALU.mult)
+            first = work.tile([P, V_WIDTH], F32, name="first")
+            nc.scalar.activation(out=first[:], in_=y[0][:], func=ACT.Copy, scale=factor[:, 0:1])
+            result = work.tile([P, V_WIDTH], F32, name="result")
+            nc.vector.scalar_tensor_tensor(
+                out=result[:],
+                in0=y[1][:],
+                scalar=factor[:, 1:2],
+                in1=first[:],
+                op0=ALU.mult,
+                op1=ALU.add,
+            )
+            nc.sync.dma_start(
+                out=out_tiles[i][:, h * V_WIDTH : (h + 1) * V_WIDTH], in_=result[:]
+            )
+
+        for half in range(2):
+            transpose_q_and_k(0, half)
+        load_q_and_k(4)
+        for h in range(N_VHEADS):
+            quantise_v(0, h)
+            load_v(1, h)
+
+        for step in range(N_UNITS + 2):
+            if step >= 2:
+                quantise_e(step - 2)
+            if step < N_UNITS:
+                scores_and_exp(step)
+            if step < 2 * (N_TILES - 1):
+                tile_ahead, half = 1 + step // 2, step % 2
+                transpose_q_and_k(tile_ahead, half)
+                if half == 1 and tile_ahead + 4 < N_TILES:
+                    load_q_and_k(tile_ahead + 4)
+            if 4 <= step < 4 + N_VHEADS:
+                quantise_v(1, step - 4)
+            if 1 <= step <= N_UNITS:
+                transpose_e(step - 1)
+            if step >= 2:
+                attend_and_combine(step - 2)

@@ -45,6 +45,7 @@ def tile_mixerdiffattention_pb_kernel(
         psum_s = ctx.enter_context(tc.psum_pool(name="psum_s", bufs=4))
         psum_t = ctx.enter_context(tc.psum_pool(name="psum_t", bufs=2))
         psum_y = ctx.enter_context(tc.psum_pool(name="psum_y", bufs=2))
+        ctx.enter_context(tc.manual_schedule())
 
         q_tiles = q_rot[0].rearrange("(i p) h d -> i p (h d)", p=P)
         k_tiles = k_rot[0].rearrange("(i p) h d -> i p (h d)", p=P)
@@ -66,10 +67,13 @@ def tile_mixerdiffattention_pb_kernel(
             nc.sync.dma_start(out=v_raw[g, h][:], in_=v_rows[g, h])
 
         load_q_and_k(0)
-        for h in range(N_VHEADS):
-            load_v(0, h)
-        for i in range(1, 4):
-            load_q_and_k(i)
+        load_q_and_k(1)
+        load_v(0, 0)
+        load_v(0, 1)
+        load_q_and_k(2)
+        load_v(0, 2)
+        load_v(0, 3)
+        load_q_and_k(3)
 
         ident_f32 = keep.tile([P, P], F32, name="ident_f32")
         make_identity(nc, ident_f32[:])
@@ -99,24 +103,26 @@ def tile_mixerdiffattention_pb_kernel(
         lam_in = keep.tile([P, 4, P], BF16, name="lam_in")
         for n, vec in enumerate((lambda_q1, lambda_q2, lambda_k1, lambda_k2)):
             nc.scalar.dma_start(out=lam_in[:, n, :], in_=vec.partition_broadcast(P))
-        lam_prod = keep.tile([P, N_GROUPS, P], F32, name="lam_prod")
-        nc.vector.tensor_tensor(
-            out=lam_prod[:], in0=lam_in[:, 0:2, :], in1=lam_in[:, 2:4, :], op=ALU.mult
-        )
-        lam_dot = keep.tile([P, N_GROUPS], F32, name="lam_dot")
-        nc.vector.tensor_reduce(out=lam_dot[:], in_=lam_prod[:], axis=AXIS.X, op=ALU.add)
-        lam_exp = keep.tile([P, N_GROUPS], F32, name="lam_exp")
-        nc.scalar.activation(out=lam_exp[:], in_=lam_dot[:], func=ACT.Exp)
         weights = keep.tile([P, N_GROUPS], F32, name="weights")
-        nc.vector.memset(weights[:, 0:1], 1.0)
-        nc.vector.tensor_scalar(
-            out=weights[:, 1:2],
-            in0=lam_exp[:, 1:2],
-            scalar1=lam_exp[:, 0:1],
-            scalar2=LAMBDA_INIT,
-            op0=ALU.subtract,
-            op1=ALU.subtract,
-        )
+
+        def compute_weights():
+            lam_prod = keep.tile([P, N_GROUPS, P], F32, name="lam_prod")
+            nc.vector.tensor_tensor(
+                out=lam_prod[:], in0=lam_in[:, 0:2, :], in1=lam_in[:, 2:4, :], op=ALU.mult
+            )
+            lam_dot = keep.tile([P, N_GROUPS], F32, name="lam_dot")
+            nc.vector.tensor_reduce(out=lam_dot[:], in_=lam_prod[:], axis=AXIS.X, op=ALU.add)
+            lam_exp = keep.tile([P, N_GROUPS], F32, name="lam_exp")
+            nc.scalar.activation(out=lam_exp[:], in_=lam_dot[:], func=ACT.Exp)
+            nc.vector.memset(weights[:, 0:1], 1.0)
+            nc.vector.tensor_scalar(
+                out=weights[:, 1:2],
+                in0=lam_exp[:, 1:2],
+                scalar1=lam_exp[:, 0:1],
+                scalar2=LAMBDA_INIT,
+                op0=ALU.subtract,
+                op1=ALU.subtract,
+            )
 
         e_bufs = []
         for n in range(2 * N_GROUPS):
@@ -250,7 +256,7 @@ def tile_mixerdiffattention_pb_kernel(
                         nc.tensor.transpose(planes[grp][:, g, t, :], e_buf[:, g, t, :], ident_bf16[:])
             for grp in range(N_GROUPS):
                 source = planes[grp][:].rearrange("p g t q -> p g q t")
-                if grp == 1 and h % 2 == 1:
+                if n_pass == 2 and grp == 1 and h % 2 == 1:
                     nc.vector.tensor_copy(out=e_grouped[unit][:, grp], in_=source)
                 else:
                     nc.scalar.copy(out=e_grouped[unit][:, grp], in_=source)
@@ -266,16 +272,19 @@ def tile_mixerdiffattention_pb_kernel(
                 in_=e_grouped[unit][:].rearrange("p a g q t -> p (a g q t)"),
             )
 
-        def attend_and_combine(unit):
-            i, h = unit // N_VHEADS, unit % N_VHEADS
+        acc = {}
+        factor = {}
+        first = {}
+
+        def attend(unit):
+            h = unit % N_VHEADS
             n_pass = passes_of(unit)
-            y = []
             for grp in range(N_GROUPS):
-                acc = psum_y.tile([P, V_WIDTH], F32, tag="y", name="acc")
+                acc[unit, grp] = psum_y.tile([P, V_WIDTH], F32, tag="y", name="acc")
                 for g in range(n_pass):
                     cols = slice((grp * n_pass + g) * P, (grp * n_pass + g + 1) * P)
                     nc.tensor.matmul_mx(
-                        out=acc[:],
+                        out=acc[unit, grp][:],
                         lhsT=e_codes[unit][:, cols].bitcast(FP8X4),
                         lhsT_scale=e_scales[unit][:, cols],
                         rhs=v_codes[:, g, h, :].bitcast(FP8X4),
@@ -283,24 +292,32 @@ def tile_mixerdiffattention_pb_kernel(
                         start=(g == 0),
                         stop=(g == n_pass - 1),
                     )
-                y.append(acc)
+
+        def compute_factors(unit):
             inverse = small.tile([P, N_GROUPS], F32, name="inverse")
-            if n_pass == 1:
+            if passes_of(unit) == 1:
                 nc.vector.reciprocal(out=inverse[:], in_=sums[unit][:, :, 0])
             else:
                 total = small.tile([P, N_GROUPS], F32, name="total")
                 nc.vector.tensor_reduce(out=total[:], in_=sums[unit][:], axis=AXIS.X, op=ALU.add)
                 nc.vector.reciprocal(out=inverse[:], in_=total[:])
-            factor = small.tile([P, N_GROUPS], F32, name="factor")
-            nc.vector.tensor_tensor(out=factor[:], in0=inverse[:], in1=weights[:], op=ALU.mult)
-            first = work.tile([P, V_WIDTH], F32, name="first")
-            nc.scalar.activation(out=first[:], in_=y[0][:], func=ACT.Copy, scale=factor[:, 0:1])
+            factor[unit] = small.tile([P, N_GROUPS], F32, name="factor")
+            nc.vector.tensor_tensor(out=factor[unit][:], in0=inverse[:], in1=weights[:], op=ALU.mult)
+
+        def scale_first_group(unit):
+            first[unit] = work.tile([P, V_WIDTH], F32, name="first")
+            nc.scalar.activation(
+                out=first[unit][:], in_=acc[unit, 0][:], func=ACT.Copy, scale=factor[unit][:, 0:1]
+            )
+
+        def add_second_group_and_store(unit):
+            i, h = unit // N_VHEADS, unit % N_VHEADS
             result = work.tile([P, V_WIDTH], F32, name="result")
             nc.vector.scalar_tensor_tensor(
                 out=result[:],
-                in0=y[1][:],
-                scalar=factor[:, 1:2],
-                in1=first[:],
+                in0=acc[unit, 1][:],
+                scalar=factor[unit][:, 1:2],
+                in1=first[unit][:],
                 op0=ALU.mult,
                 op1=ALU.add,
             )
@@ -311,23 +328,31 @@ def tile_mixerdiffattention_pb_kernel(
         for half in range(2):
             transpose_q_and_k(0, half)
         load_q_and_k(4)
-        for h in range(N_VHEADS):
-            quantise_v(0, h)
-            load_v(1, h)
+        compute_weights()
 
-        for step in range(N_UNITS + 2):
-            if step >= 2:
-                quantise_e(step - 2)
-            if step < N_UNITS:
+        def live(unit):
+            return 0 <= unit < N_UNITS
+
+        for step in range(N_UNITS + 4):
+            if live(step):
                 scores_and_exp(step)
+            if live(step - 4):
+                add_second_group_and_store(step - 4)
+            if live(step - 2):
+                quantise_e(step - 2)
+                compute_factors(step - 2)
+            if step < N_VHEADS:
+                quantise_v(0, step)
+                load_v(1, step)
             if step < 2 * (N_TILES - 1):
                 tile_ahead, half = 1 + step // 2, step % 2
                 transpose_q_and_k(tile_ahead, half)
                 if half == 1 and tile_ahead + 4 < N_TILES:
                     load_q_and_k(tile_ahead + 4)
-            if 4 <= step < 4 + N_VHEADS:
-                quantise_v(1, step - 4)
-            if 1 <= step <= N_UNITS:
+            if 8 <= step < 8 + N_VHEADS:
+                quantise_v(1, step - 8)
+            if live(step - 1):
                 transpose_e(step - 1)
-            if step >= 2:
-                attend_and_combine(step - 2)
+            if live(step - 3):
+                attend(step - 3)
+                scale_first_group(step - 3)

@@ -6,6 +6,7 @@ from concourse.masks import make_identity
 
 F32 = mybir.dt.float32
 BF16 = mybir.dt.bfloat16
+I32 = mybir.dt.int32
 U32 = mybir.dt.uint32
 U8 = mybir.dt.uint8
 FP8X4 = mybir.dt.float8_e4m3fn_x4
@@ -45,7 +46,6 @@ def tile_mixerdiffattention_pb_kernel(
         psum_s = ctx.enter_context(tc.psum_pool(name="psum_s", bufs=4))
         psum_t = ctx.enter_context(tc.psum_pool(name="psum_t", bufs=2))
         psum_y = ctx.enter_context(tc.psum_pool(name="psum_y", bufs=2))
-        ctx.enter_context(tc.manual_schedule())
 
         q_tiles = q_rot[0].rearrange("(i p) h d -> i p (h d)", p=P)
         k_tiles = k_rot[0].rearrange("(i p) h d -> i p (h d)", p=P)
@@ -127,7 +127,7 @@ def tile_mixerdiffattention_pb_kernel(
         e_bufs = []
         for n in range(2 * N_GROUPS):
             e_buf = keep.tile([P, 2, PACK, P], BF16, name="e_buf%d" % n)
-            nc.vector.memset(e_buf[:], 0.0)
+            nc.vector.memset(e_buf[:].bitcast(I32), 0)
             e_bufs.append(e_buf)
 
         q_t = keep.tile([P, N_TILES, N_HEADS, P], F32, name="q_t")
@@ -210,35 +210,25 @@ def tile_mixerdiffattention_pb_kernel(
                         )
                     banks.append(s)
                     widths.append(width)
-                top = small.tile([P, n_pass], F32, name="top")
+                scaled = work.tile([P, n_pass, PACK, P], F32, name="scaled")
+                low = small.tile([P, n_pass], F32, name="low")
                 for g in range(n_pass):
-                    nc.vector.tensor_reduce(
-                        out=top[:, g : g + 1],
-                        in_=banks[g][:, :, 0 : widths[g]],
-                        axis=AXIS.XY,
-                        op=ALU.max,
-                    )
-                shift = small.tile([P, 1], F32, name="shift")
-                if n_pass == 1:
                     nc.vector.tensor_scalar(
-                        out=shift[:], in0=top[:, 0:1], scalar1=-SCALE, scalar2=None, op0=ALU.mult
-                    )
-                else:
-                    nc.vector.tensor_scalar(
-                        out=shift[:],
-                        in0=top[:, 0:1],
-                        scalar1=top[:, 1:2],
-                        scalar2=-SCALE,
-                        op0=ALU.max,
-                        op1=ALU.mult,
+                        out=scaled[:, g, :, 0 : widths[g]],
+                        in0=banks[g][:, :, 0 : widths[g]],
+                        scalar1=-SCALE,
+                        scalar2=(None if g == 0 else low[:, g - 1 : g]),
+                        op0=ALU.mult,
+                        op1=ALU.min,
+                        accum_out=low[:, g : g + 1],
                     )
                 for g in range(n_pass):
                     nc.scalar.activation(
                         out=e_buf[:, g, :, 0 : widths[g]],
-                        in_=banks[g][:, :, 0 : widths[g]],
+                        in_=scaled[:, g, :, 0 : widths[g]],
                         func=ACT.Exp,
-                        bias=shift[:, 0:1],
-                        scale=SCALE,
+                        bias=low[:, n_pass - 1 : n_pass],
+                        scale=-1.0,
                         accum_out=sums[unit][:, grp, g : g + 1],
                     )
 

@@ -15,12 +15,14 @@ ACT = mybir.ActivationFunctionType
 AXIS = mybir.AxisListType
 
 P = 128
+PAIR = 2
+HALF = 256
+RUN = 64
 PACK = 4
 K_PASS = P * PACK
 SEQ = 1024
 N_TILES = SEQ // P
 TILES_PER_PASS = K_PASS // P
-RUN = P // PACK
 N_HEADS = 8
 N_GROUPS = 2
 N_VHEADS = 4
@@ -30,9 +32,10 @@ SCALE = 1.0 / math.sqrt(HEAD_DIM)
 LAMBDA_INIT = 0.8 - 0.6 * math.exp(-0.3 * 0)
 MASKED = -1.0e30
 N_UNITS = N_TILES * N_VHEADS
+N_ITEMS = N_UNITS * N_GROUPS
 
 FLOPS = N_HEADS * (512 * 512 + 512 * 1024) * 2 * (HEAD_DIM + V_WIDTH)
-
+N_E_BUFS = 4
 
 def tile_mixerdiffattention_pb_kernel(
     tc, q_rot, k_rot, v, lambda_q1, lambda_k1, lambda_q2, lambda_k2, out
@@ -41,8 +44,8 @@ def tile_mixerdiffattention_pb_kernel(
     with ExitStack() as ctx:
         keep = ctx.enter_context(tc.tile_pool(name="keep", bufs=1))
         raw = ctx.enter_context(tc.tile_pool(name="raw", bufs=4))
-        work = ctx.enter_context(tc.tile_pool(name="work", bufs=3))
-        small = ctx.enter_context(tc.tile_pool(name="small", bufs=6))
+        work = ctx.enter_context(tc.tile_pool(name="work", bufs=4))
+        small = ctx.enter_context(tc.tile_pool(name="small", bufs=8))
         psum_s = ctx.enter_context(tc.psum_pool(name="psum_s", bufs=4))
         psum_t = ctx.enter_context(tc.psum_pool(name="psum_t", bufs=2))
         psum_y = ctx.enter_context(tc.psum_pool(name="psum_y", bufs=2))
@@ -66,12 +69,18 @@ def tile_mixerdiffattention_pb_kernel(
             v_raw[g, h] = raw.tile([P, PACK, V_WIDTH], BF16, name="v_raw")
             nc.sync.dma_start(out=v_raw[g, h][:], in_=v_rows[g, h])
 
+        lam_q = keep.tile([N_GROUPS, P], BF16, name="lam_q")
+        lam_k = keep.tile([N_GROUPS, P], BF16, name="lam_k")
+        for n, (vec_q, vec_k) in enumerate(((lambda_q1, lambda_k1), (lambda_q2, lambda_k2))):
+            nc.scalar.dma_start(out=lam_q[n : n + 1, :], in_=vec_q.unsqueeze(0))
+            nc.scalar.dma_start(out=lam_k[n : n + 1, :], in_=vec_k.unsqueeze(0))
+
         load_q_and_k(0)
-        load_q_and_k(1)
         load_v(0, 0)
+        load_q_and_k(1)
         load_v(0, 1)
-        load_q_and_k(2)
         load_v(0, 2)
+        load_q_and_k(2)
         load_v(0, 3)
         load_q_and_k(3)
 
@@ -81,8 +90,8 @@ def tile_mixerdiffattention_pb_kernel(
         make_identity(nc, ident_bf16[:])
         to_planes = keep.tile([P, P], F32, name="to_planes")
         nc.vector.tensor_copy(
-            out=to_planes[:].rearrange("p (t r) -> p t r", t=PACK),
-            in_=ident_f32[:].rearrange("p (r t) -> p t r", t=PACK),
+            out=to_planes[:].rearrange("p (u r e) -> p u r e", u=PAIR, e=PAIR),
+            in_=ident_f32[:].rearrange("p (r u e) -> p u r e", u=PAIR, e=PAIR),
         )
         mask_f32 = keep.tile([P, P], F32, name="mask_f32")
         nc.gpsimd.memset(mask_f32[:], 0.0)
@@ -95,28 +104,43 @@ def tile_mixerdiffattention_pb_kernel(
             pattern=[[-1, P]],
             channel_multiplier=1,
         )
-        mask = keep.tile([P, PACK, RUN], BF16, name="mask")
+        mask = keep.tile([P, PAIR, RUN], BF16, name="mask")
         nc.vector.tensor_copy(
-            out=mask[:], in_=mask_f32[:].rearrange("p (r t) -> p t r", t=PACK)
+            out=mask[:].rearrange("p u (r e) -> p u r e", e=PAIR),
+            in_=mask_f32[:].rearrange("p (r u e) -> p u r e", u=PAIR, e=PAIR),
         )
+        e_bufs = []
+        for n in range(N_E_BUFS):
+            e_buf = keep.tile([P, 2, PAIR, HALF], BF16, name="e_buf%d" % n)
+            nc.gpsimd.memset(e_buf[:].bitcast(I32), 0)
+            e_bufs.append(e_buf)
 
-        lam_in = keep.tile([P, 4, P], BF16, name="lam_in")
-        for n, vec in enumerate((lambda_q1, lambda_q2, lambda_k1, lambda_k2)):
-            nc.scalar.dma_start(out=lam_in[:, n, :], in_=vec.partition_broadcast(P))
-        weights = keep.tile([P, N_GROUPS], F32, name="weights")
+        ones = keep.tile([P, P], F32, name="ones")
+        nc.gpsimd.memset(ones[:], 1.0)
+        lam_dot = keep.tile([P, 1], F32, name="lam_dot")
+        nc.gpsimd.memset(lam_dot[:], 0.0)
+        minus_lam = keep.tile([P, 1], F32, name="minus_lam")
 
-        def compute_weights():
-            lam_prod = keep.tile([P, N_GROUPS, P], F32, name="lam_prod")
-            nc.vector.tensor_tensor(
-                out=lam_prod[:], in0=lam_in[:, 0:2, :], in1=lam_in[:, 2:4, :], op=ALU.mult
+        def compute_lam():
+            lam_prod = keep.tile([N_GROUPS, P], F32, name="lam_prod")
+            nc.vector.tensor_tensor(out=lam_prod[:], in0=lam_q[:], in1=lam_k[:], op=ALU.mult)
+            nc.vector.tensor_reduce(
+                out=lam_dot[0:N_GROUPS, :], in_=lam_prod[:], axis=AXIS.X, op=ALU.add
             )
-            lam_dot = keep.tile([P, N_GROUPS], F32, name="lam_dot")
-            nc.vector.tensor_reduce(out=lam_dot[:], in_=lam_prod[:], axis=AXIS.X, op=ALU.add)
-            lam_exp = keep.tile([P, N_GROUPS], F32, name="lam_exp")
-            nc.scalar.activation(out=lam_exp[:], in_=lam_dot[:], func=ACT.Exp)
-            nc.vector.memset(weights[:, 0:1], 1.0)
+            lam_diag = keep.tile([P, N_GROUPS], F32, name="lam_diag")
             nc.vector.tensor_scalar(
-                out=weights[:, 1:2],
+                out=lam_diag[:],
+                in0=ident_f32[:, 0:N_GROUPS],
+                scalar1=lam_dot[:],
+                scalar2=None,
+                op0=ALU.mult,
+            )
+            lam_sum = psum_t.tile([P, N_GROUPS], F32, tag="t", name="lam_sum")
+            nc.tensor.matmul(out=lam_sum[:], lhsT=ones[:], rhs=lam_diag[:], start=True, stop=True)
+            lam_exp = keep.tile([P, N_GROUPS], F32, name="lam_exp")
+            nc.scalar.activation(out=lam_exp[:], in_=lam_sum[:], func=ACT.Exp)
+            nc.vector.tensor_scalar(
+                out=minus_lam[:],
                 in0=lam_exp[:, 1:2],
                 scalar1=lam_exp[:, 0:1],
                 scalar2=LAMBDA_INIT,
@@ -124,225 +148,266 @@ def tile_mixerdiffattention_pb_kernel(
                 op1=ALU.subtract,
             )
 
-        e_bufs = []
-        for n in range(2 * N_GROUPS):
-            e_buf = keep.tile([P, 2, PACK, P], BF16, name="e_buf%d" % n)
-            nc.vector.memset(e_buf[:].bitcast(I32), 0)
-            e_bufs.append(e_buf)
-
-        q_t = keep.tile([P, N_TILES, N_HEADS, P], F32, name="q_t")
-        k_t = keep.tile([P, N_HEADS, SEQ], F32, name="k_t")
-        q_pairs = q_t[:].bitcast(BF16).rearrange("w i h (q e) -> w i h q e", e=2)
+        q_t = keep.tile([P, N_TILES, N_GROUPS, N_VHEADS, P], F32, name="q_t")
+        k_t = keep.tile([P, N_GROUPS, N_VHEADS, SEQ], F32, name="k_t")
+        q_pairs = q_t[:].bitcast(BF16).rearrange("w i a h (q e) -> w i a h q e", e=2)
         k_pairs = k_t[:].bitcast(BF16).rearrange(
-            "w h (g t p e) -> w h g t p e", t=PACK, p=P, e=2
+            "w a h (g u x e) -> w a h g u x e", u=PAIR, x=HALF, e=2
         )
-        k_words = k_t[:].rearrange("w h (g t p) -> w h g t p", t=PACK, p=P)
+        k_words = k_t[:].rearrange("w a h (g u x) -> w a h g u x", u=PAIR, x=HALF)
 
         def transpose_q_and_k(i, half):
-            heads = slice(4 * half, 4 * half + 4)
+            q_bank = psum_s.tile([P, N_GROUPS, 2, P], F32, tag="s", name="q_bank")
+            k_bank = psum_s.tile([P, N_GROUPS, 2, P], F32, tag="s", name="k_bank")
+            for bank, source, order in (
+                (q_bank, q_raw[i], ident_f32),
+                (k_bank, k_raw[i], to_planes),
+            ):
+                for grp in range(N_GROUPS):
+                    for n in range(2):
+                        head = N_VHEADS * grp + 2 * half + n
+                        words = slice(head * P, (head + 1) * P)
+                        nc.tensor.transpose(
+                            bank[:, grp, n, :], source[:].bitcast(F32)[:, words], order[:]
+                        )
+            pair = slice(2 * half, 2 * half + 2)
+            nc.scalar.copy(out=q_t[:, i, :, pair, :], in_=q_bank[:])
             g, column = i // TILES_PER_PASS, RUN * (i % TILES_PER_PASS)
-            q_bank = psum_s.tile([P, 4, P], F32, tag="s", name="q_bank")
-            k_bank = psum_s.tile([P, 4, P], F32, tag="s", name="k_bank")
-            for a in range(4):
-                words = slice((4 * half + a) * P, (4 * half + a + 1) * P)
-                nc.tensor.transpose(q_bank[:, a, :], q_raw[i][:].bitcast(F32)[:, words], ident_f32[:])
-            for a in range(4):
-                words = slice((4 * half + a) * P, (4 * half + a + 1) * P)
-                nc.tensor.transpose(k_bank[:, a, :], k_raw[i][:].bitcast(F32)[:, words], to_planes[:])
-            nc.scalar.copy(out=q_t[:, i, heads, :], in_=q_bank[:])
-            nc.vector.tensor_copy(
-                out=k_words[:, heads, g, :, column : column + RUN],
-                in_=k_bank[:].rearrange("w a (t r) -> w a t r", t=PACK),
-            )
+            for grp in range(N_GROUPS):
+                k_out = k_words[:, grp, pair, g, :, column : column + RUN]
+                k_in = k_bank[:, grp].rearrange("w n (u x) -> w n u x", u=PAIR)
+                nc.vector.tensor_copy(out=k_out, in_=k_in)
 
         v_codes = keep.tile([P, 2, N_VHEADS, V_WIDTH], U32, name="v_codes", align_bytes=64)
         v_scales = keep.tile([P, 2, N_VHEADS, V_WIDTH], U8, name="v_scales", align_bytes=64)
+        v_groups = {}
+
+        def group_v(g, h, on_vector):
+            v_groups[g, h] = work.tile([P, V_WIDTH, PACK], BF16, name="v_grouped", align_bytes=64)
+            out_ap = v_groups[g, h][:].rearrange("p (c n) j -> p c j n", n=4)
+            in_ap = v_raw[g, h][:].rearrange("p j (c n) -> p c j n", n=4)
+            if on_vector:
+                nc.vector.tensor_copy(out=out_ap, in_=in_ap)
+            else:
+                nc.gpsimd.tensor_scalar(
+                    out=out_ap, in0=in_ap, scalar1=1.0, scalar2=0.0, op0=ALU.mult, op1=ALU.add
+                )
 
         def quantise_v(g, h):
-            v_grouped = work.tile([P, V_WIDTH, PACK], BF16, name="v_grouped", align_bytes=64)
-            nc.vector.tensor_copy(
-                out=v_grouped[:].rearrange("p (c n) j -> p c j n", n=4),
-                in_=v_raw[g, h][:].rearrange("p j (c n) -> p c j n", n=4),
-            )
             nc.vector.quantize_mx(
                 out=v_codes[:, g, h, :].bitcast(FP8X4),
                 scales=v_scales[:, g, h, :],
-                in_=v_grouped[:].rearrange("p c j -> p (c j)"),
+                in_=v_groups[g, h][:].rearrange("p c j -> p (c j)"),
             )
 
+        def tile_head_group(item):
+            unit = item // N_GROUPS
+            return unit // N_VHEADS, unit % N_VHEADS, item % N_GROUPS
+
+        def passes_of(item):
+            return (item // N_GROUPS // N_VHEADS) // TILES_PER_PASS + 1
+
+        banks = {}
+        scaled = {}
+        low = {}
+        e_of = {}
         sums = {}
         planes = {}
         e_grouped = {}
         e_codes = {}
         e_scales = {}
-
-        def passes_of(unit):
-            return (unit // N_VHEADS) // TILES_PER_PASS + 1
-
-        def scores_and_exp(unit):
-            i, h = unit // N_VHEADS, unit % N_VHEADS
-            n_pass = passes_of(unit)
-            sums[unit] = small.tile([P, N_GROUPS, n_pass], F32, name="sums")
-            for grp in range(N_GROUPS):
-                head = N_VHEADS * grp + h
-                e_buf = e_bufs[N_GROUPS * (unit % 2) + grp]
-                banks = []
-                widths = []
-                for g in range(n_pass):
-                    last = g == n_pass - 1
-                    width = RUN * (i % TILES_PER_PASS + 1) if last else P
-                    s = psum_s.tile([P, PACK, P], F32, tag="s", name="s")
-                    for parity in range(2):
-                        nc.tensor.matmul(
-                            out=s[:, :, 0:width],
-                            lhsT=q_pairs[:, i, head, :, parity],
-                            rhs=k_pairs[:, head, g, :, 0:width, parity],
-                            start=(parity == 0),
-                            stop=(parity == 1 and not last),
-                        )
-                    if last:
-                        nc.tensor.matmul(
-                            out=s[:, :, width - RUN : width],
-                            lhsT=ident_bf16[:],
-                            rhs=mask[:],
-                            start=False,
-                            stop=True,
-                        )
-                    banks.append(s)
-                    widths.append(width)
-                scaled = work.tile([P, n_pass, PACK, P], F32, name="scaled")
-                low = small.tile([P, n_pass], F32, name="low")
-                for g in range(n_pass):
-                    nc.vector.tensor_scalar(
-                        out=scaled[:, g, :, 0 : widths[g]],
-                        in0=banks[g][:, :, 0 : widths[g]],
-                        scalar1=-SCALE,
-                        scalar2=(None if g == 0 else low[:, g - 1 : g]),
-                        op0=ALU.mult,
-                        op1=ALU.min,
-                        accum_out=low[:, g : g + 1],
-                    )
-                for g in range(n_pass):
-                    nc.scalar.activation(
-                        out=e_buf[:, g, :, 0 : widths[g]],
-                        in_=scaled[:, g, :, 0 : widths[g]],
-                        func=ACT.Exp,
-                        bias=low[:, n_pass - 1 : n_pass],
-                        scale=-1.0,
-                        accum_out=sums[unit][:, grp, g : g + 1],
-                    )
-
-        def transpose_e(unit):
-            h = unit % N_VHEADS
-            n_pass = passes_of(unit)
-            e_grouped[unit] = work.tile(
-                [P, N_GROUPS, n_pass, P, PACK], BF16, name="e_grouped", align_bytes=64
-            )
-            for grp in range(N_GROUPS):
-                e_buf = e_bufs[N_GROUPS * (unit % 2) + grp]
-                planes[grp] = psum_t.tile([P, n_pass, PACK, P], BF16, tag="t", name="planes")
-                for g in range(n_pass):
-                    for t in range(PACK):
-                        nc.tensor.transpose(planes[grp][:, g, t, :], e_buf[:, g, t, :], ident_bf16[:])
-            for grp in range(N_GROUPS):
-                source = planes[grp][:].rearrange("p g t q -> p g q t")
-                if n_pass == 2 and grp == 1 and h % 2 == 1:
-                    nc.vector.tensor_copy(out=e_grouped[unit][:, grp], in_=source)
-                else:
-                    nc.scalar.copy(out=e_grouped[unit][:, grp], in_=source)
-
-        def quantise_e(unit):
-            n_pass = passes_of(unit)
-            width = N_GROUPS * n_pass * P
-            e_codes[unit] = work.tile([P, width], U32, name="e_codes", align_bytes=64)
-            e_scales[unit] = work.tile([P, width], U8, name="e_scales", align_bytes=64)
-            nc.vector.quantize_mx(
-                out=e_codes[unit][:].bitcast(FP8X4),
-                scales=e_scales[unit][:],
-                in_=e_grouped[unit][:].rearrange("p a g q t -> p (a g q t)"),
-            )
-
         acc = {}
+        inverse = {}
         factor = {}
         first = {}
 
-        def attend(unit):
-            h = unit % N_VHEADS
-            n_pass = passes_of(unit)
-            for grp in range(N_GROUPS):
-                acc[unit, grp] = psum_y.tile([P, V_WIDTH], F32, tag="y", name="acc")
-                for g in range(n_pass):
-                    cols = slice((grp * n_pass + g) * P, (grp * n_pass + g + 1) * P)
-                    nc.tensor.matmul_mx(
-                        out=acc[unit, grp][:],
-                        lhsT=e_codes[unit][:, cols].bitcast(FP8X4),
-                        lhsT_scale=e_scales[unit][:, cols],
-                        rhs=v_codes[:, g, h, :].bitcast(FP8X4),
-                        rhs_scale=v_scales[:, g, h, :],
-                        start=(g == 0),
-                        stop=(g == n_pass - 1),
+        def widths_of(item):
+            i = item // N_GROUPS // N_VHEADS
+            return [HALF] * (i // TILES_PER_PASS) + [RUN * (i % TILES_PER_PASS + 1)]
+
+        def score(item):
+            i, h, grp = tile_head_group(item)
+            widths = widths_of(item)
+            banks[item] = []
+            for g, width in enumerate(widths):
+                last = g == len(widths) - 1
+                s = psum_s.tile([P, PAIR, HALF], F32, tag="s", name="s")
+                for parity in range(2):
+                    nc.tensor.matmul(
+                        out=s[:, :, 0:width],
+                        lhsT=q_pairs[:, i, grp, h, :, parity],
+                        rhs=k_pairs[:, grp, h, g, :, 0:width, parity],
+                        start=(parity == 0),
+                        stop=(parity == 1 and not last),
+                    )
+                if last:
+                    nc.tensor.matmul(
+                        out=s[:, :, width - RUN : width],
+                        lhsT=ident_bf16[:],
+                        rhs=mask[:],
+                        start=False,
+                        stop=True,
+                    )
+                banks[item].append(s)
+
+        def find_maximum(item, n):
+            widths = widths_of(item)
+            if n >= len(widths):
+                return
+            if n == 0:
+                scaled[item] = work.tile([P, len(widths), PAIR, HALF], F32, name="scaled")
+                low[item] = small.tile([P, 2], F32, name="low")
+            nc.vector.tensor_scalar(
+                out=scaled[item][:, n, :, 0 : widths[n]],
+                in0=banks[item][n][:, :, 0 : widths[n]],
+                scalar1=-SCALE,
+                scalar2=(None if n == 0 else low[item][:, n - 1 : n]),
+                op0=ALU.mult,
+                op1=ALU.min,
+                accum_out=low[item][:, n : n + 1],
+            )
+
+        def exponential(item):
+            i, h, grp = tile_head_group(item)
+            unit = item // N_GROUPS
+            n_pass = passes_of(item)
+            if grp == 0:
+                sums[unit] = small.tile([P, N_GROUPS, n_pass], F32, name="sums")
+            e_of[item] = e_bufs[item % N_E_BUFS]
+            for g, width in enumerate(widths_of(item)):
+                nc.scalar.activation(
+                    out=e_of[item][:, g, :, 0:width],
+                    in_=scaled[item][:, g, :, 0:width],
+                    func=ACT.Exp,
+                    bias=low[item][:, n_pass - 1 : n_pass],
+                    scale=-1.0,
+                    accum_out=sums[unit][:, grp, g : g + 1],
+                )
+
+        def transpose_e(item):
+            n_pass = passes_of(item)
+            planes[item] = psum_t.tile([P, n_pass, PAIR, P], F32, tag="t", name="planes")
+            e_buf = e_of.pop(item)
+            for g in range(n_pass):
+                for u in range(PAIR):
+                    nc.tensor.transpose(
+                        planes[item][:, g, u, :], e_buf[:, g, u, :].bitcast(F32), ident_f32[:]
                     )
 
+        def group_e(item):
+            n_pass = passes_of(item)
+            e_grouped[item] = work.tile([P, n_pass, P, PAIR], F32, name="e_grouped", align_bytes=64)
+            nc.scalar.copy(out=e_grouped[item][:], in_=planes[item][:].rearrange("p g u q -> p g q u"))
+
+        def quantise_e(item):
+            width = passes_of(item) * P
+            e_codes[item] = work.tile([P, width], U32, name="e_codes", align_bytes=64)
+            e_scales[item] = work.tile([P, width], U8, name="e_scales", align_bytes=64)
+            nc.vector.quantize_mx(
+                out=e_codes[item][:].bitcast(FP8X4),
+                scales=e_scales[item][:],
+                in_=e_grouped[item][:].rearrange("p g q u -> p (g q u)").bitcast(BF16),
+            )
+
+        def attend(item):
+            i, h, grp = tile_head_group(item)
+            n_pass = passes_of(item)
+            acc[item] = psum_y.tile([P, V_WIDTH], F32, tag="y", name="acc")
+            for g in range(n_pass):
+                cols = slice(g * P, (g + 1) * P)
+                nc.tensor.matmul_mx(
+                    out=acc[item][:],
+                    lhsT=e_codes[item][:, cols].bitcast(FP8X4),
+                    lhsT_scale=e_scales[item][:, cols],
+                    rhs=v_codes[:, g, h, :].bitcast(FP8X4),
+                    rhs_scale=v_scales[:, g, h, :],
+                    start=(g == 0),
+                    stop=(g == n_pass - 1),
+                )
+
         def compute_factors(unit):
-            inverse = small.tile([P, N_GROUPS], F32, name="inverse")
-            if passes_of(unit) == 1:
-                nc.vector.reciprocal(out=inverse[:], in_=sums[unit][:, :, 0])
+            inverse[unit] = small.tile([P, N_GROUPS], F32, name="inverse")
+            if passes_of(N_GROUPS * unit) == 1:
+                total = sums[unit][:, :, 0]
             else:
-                total = small.tile([P, N_GROUPS], F32, name="total")
-                nc.vector.tensor_reduce(out=total[:], in_=sums[unit][:], axis=AXIS.X, op=ALU.add)
-                nc.vector.reciprocal(out=inverse[:], in_=total[:])
-            factor[unit] = small.tile([P, N_GROUPS], F32, name="factor")
-            nc.vector.tensor_tensor(out=factor[unit][:], in0=inverse[:], in1=weights[:], op=ALU.mult)
-
-        def scale_first_group(unit):
-            first[unit] = work.tile([P, V_WIDTH], F32, name="first")
-            nc.scalar.activation(
-                out=first[unit][:], in_=acc[unit, 0][:], func=ACT.Copy, scale=factor[unit][:, 0:1]
+                both = small.tile([P, N_GROUPS], F32, name="both")
+                nc.gpsimd.tensor_tensor(
+                    out=both[:], in0=sums[unit][:, :, 0], in1=sums[unit][:, :, 1], op=ALU.add
+                )
+                total = both[:]
+            nc.vector.reciprocal(out=inverse[unit][:], in_=total)
+            factor[unit] = small.tile([P, 1], F32, name="factor")
+            nc.gpsimd.tensor_tensor(
+                out=factor[unit][:], in0=inverse[unit][:, 1:2], in1=minus_lam[:], op=ALU.mult
             )
 
-        def add_second_group_and_store(unit):
-            i, h = unit // N_VHEADS, unit % N_VHEADS
-            result = work.tile([P, V_WIDTH], F32, name="result")
-            nc.vector.scalar_tensor_tensor(
-                out=result[:],
-                in0=acc[unit, 1][:],
-                scalar=factor[unit][:, 1:2],
-                in1=first[unit][:],
-                op0=ALU.mult,
-                op1=ALU.add,
-            )
-            nc.sync.dma_start(
-                out=out_tiles[i][:, h * V_WIDTH : (h + 1) * V_WIDTH], in_=result[:]
-            )
+        def combine(item):
+            i, h, grp = tile_head_group(item)
+            unit = item // N_GROUPS
+            if grp == 0:
+                first[unit] = work.tile([P, V_WIDTH], F32, name="first")
+                nc.scalar.activation(
+                    out=first[unit][:], in_=acc[item][:], func=ACT.Copy, scale=inverse[unit][:, 0:1]
+                )
+            else:
+                result = work.tile([P, V_WIDTH], F32, name="result")
+                nc.vector.scalar_tensor_tensor(
+                    out=result[:],
+                    in0=acc[item][:],
+                    scalar=factor[unit][:],
+                    in1=first[unit][:],
+                    op0=ALU.mult,
+                    op1=ALU.add,
+                )
+                nc.sync.dma_start(
+                    out=out_tiles[i][:, h * V_WIDTH : (h + 1) * V_WIDTH], in_=result[:]
+                )
 
-        for half in range(2):
-            transpose_q_and_k(0, half)
+        ctx.enter_context(tc.manual_schedule())
+        transpose_q_and_k(0, 0)
+        transpose_q_and_k(0, 1)
+        group_v(0, 0, True)
+        group_v(0, 1, True)
+        quantise_v(0, 0)
         load_q_and_k(4)
-        compute_weights()
 
-        def live(unit):
-            return 0 <= unit < N_UNITS
+        def live(item):
+            return 0 <= item < N_ITEMS
 
-        for step in range(N_UNITS + 4):
+        for step in range(N_ITEMS + 7):
             if live(step):
-                scores_and_exp(step)
-            if live(step - 4):
-                add_second_group_and_store(step - 4)
+                score(step)
+                find_maximum(step, 0)
+            if live(step - 3):
+                quantise_e(step - 3)
+            if live(step):
+                find_maximum(step, 1)
             if live(step - 2):
-                quantise_e(step - 2)
-                compute_factors(step - 2)
-            if step < N_VHEADS:
-                quantise_v(0, step)
-                load_v(1, step)
-            if step < 2 * (N_TILES - 1):
-                tile_ahead, half = 1 + step // 2, step % 2
+                transpose_e(step - 2)
+                group_e(step - 2)
+            if step == 3:
+                compute_lam()
+            if live(step - 3) and step % 2 == 0:
+                compute_factors((step - 3) // 2)
+            if step % 2 == 1 and step < 4 * (N_TILES - 1):
+                tile_ahead, half = 1 + step // 4, (step // 2) % 2
                 transpose_q_and_k(tile_ahead, half)
                 if half == 1 and tile_ahead + 4 < N_TILES:
                     load_q_and_k(tile_ahead + 4)
-            if 8 <= step < 8 + N_VHEADS:
-                quantise_v(1, step - 8)
-            if live(step - 1):
-                transpose_e(step - 1)
-            if live(step - 3):
-                attend(step - 3)
-                scale_first_group(step - 3)
+            if step < 2:
+                group_v(0, 2 + step, False)
+            if step in (2, 4, 6, 8):
+                load_v(1, step // 2 - 1)
+            if step == 2:
+                quantise_v(0, 1)
+            if step in (8, 10):
+                quantise_v(0, step // 2 - 2)
+            if 12 <= step < 28 and step % 4 == 0:
+                group_v(1, (step - 12) // 4, False)
+            if 20 <= step < 36 and step % 4 == 0:
+                quantise_v(1, (step - 20) // 4)
+            if live(step - 6):
+                attend(step - 6)
+                combine(step - 6)
+            if live(step):
+                exponential(step)

@@ -149,12 +149,12 @@ def tile_mixerdiffattention_pb_kernel(
             )
 
         q_t = keep.tile([P, N_TILES, N_GROUPS, N_VHEADS, P], F32, name="q_t")
-        k_t = keep.tile([P, N_GROUPS, N_VHEADS, SEQ], F32, name="k_t")
+        k_t = keep.tile([P, 2, N_GROUPS, 2, SEQ], F32, name="k_t")
         q_pairs = q_t[:].bitcast(BF16).rearrange("w i a h (q e) -> w i a h q e", e=2)
         k_pairs = k_t[:].bitcast(BF16).rearrange(
-            "w a h (g u x e) -> w a h g u x e", u=PAIR, x=HALF, e=2
+            "w f a n (g u x e) -> w f a n g u x e", u=PAIR, x=HALF, e=2
         )
-        k_words = k_t[:].rearrange("w a h (g u x) -> w a h g u x", u=PAIR, x=HALF)
+        k_words = k_t[:].rearrange("w f a n (g u x) -> w f (a n) g u x", u=PAIR, x=HALF)
 
         def transpose_q_and_k(i, half):
             q_bank = psum_s.tile([P, N_GROUPS, 2, P], F32, tag="s", name="q_bank")
@@ -173,10 +173,9 @@ def tile_mixerdiffattention_pb_kernel(
             pair = slice(2 * half, 2 * half + 2)
             nc.scalar.copy(out=q_t[:, i, :, pair, :], in_=q_bank[:])
             g, column = i // TILES_PER_PASS, RUN * (i % TILES_PER_PASS)
-            for grp in range(N_GROUPS):
-                k_out = k_words[:, grp, pair, g, :, column : column + RUN]
-                k_in = k_bank[:, grp].rearrange("w n (u x) -> w n u x", u=PAIR)
-                nc.vector.tensor_copy(out=k_out, in_=k_in)
+            k_out = k_words[:, half, :, g, :, column : column + RUN]
+            k_in = k_bank[:].rearrange("w a n (u x) -> w (a n) u x", u=PAIR)
+            nc.vector.tensor_copy(out=k_out, in_=k_in)
 
         v_codes = keep.tile([P, 2, N_VHEADS, V_WIDTH], U32, name="v_codes", align_bytes=64)
         v_scales = keep.tile([P, 2, N_VHEADS, V_WIDTH], U8, name="v_scales", align_bytes=64)
@@ -200,12 +199,8 @@ def tile_mixerdiffattention_pb_kernel(
                 in_=v_groups[g, h][:].rearrange("p c j -> p (c j)"),
             )
 
-        def tile_head_group(item):
-            unit = item // N_GROUPS
-            return unit // N_VHEADS, unit % N_VHEADS, item % N_GROUPS
-
-        def passes_of(item):
-            return (item // N_GROUPS // N_VHEADS) // TILES_PER_PASS + 1
+        def passes_of(unit):
+            return (unit // N_VHEADS) // TILES_PER_PASS + 1
 
         banks = {}
         scaled = {}
@@ -221,14 +216,14 @@ def tile_mixerdiffattention_pb_kernel(
         factor = {}
         first = {}
 
-        def widths_of(item):
-            i = item // N_GROUPS // N_VHEADS
+        def widths_of(unit):
+            i = unit // N_VHEADS
             return [HALF] * (i // TILES_PER_PASS) + [RUN * (i % TILES_PER_PASS + 1)]
 
-        def score(item):
-            i, h, grp = tile_head_group(item)
-            widths = widths_of(item)
-            banks[item] = []
+        def score(unit, grp):
+            i, h = unit // N_VHEADS, unit % N_VHEADS
+            widths = widths_of(unit)
+            banks[unit, grp] = []
             for g, width in enumerate(widths):
                 last = g == len(widths) - 1
                 s = psum_s.tile([P, PAIR, HALF], F32, tag="s", name="s")
@@ -236,7 +231,7 @@ def tile_mixerdiffattention_pb_kernel(
                     nc.tensor.matmul(
                         out=s[:, :, 0:width],
                         lhsT=q_pairs[:, i, grp, h, :, parity],
-                        rhs=k_pairs[:, grp, h, g, :, 0:width, parity],
+                        rhs=k_pairs[:, h // 2, grp, h % 2, g, :, 0:width, parity],
                         start=(parity == 0),
                         stop=(parity == 1 and not last),
                     )
@@ -248,77 +243,91 @@ def tile_mixerdiffattention_pb_kernel(
                         start=False,
                         stop=True,
                     )
-                banks[item].append(s)
+                banks[unit, grp].append(s)
 
-        def find_maximum(item, n):
-            widths = widths_of(item)
+        def find_maximum(unit, grp, n):
+            widths = widths_of(unit)
             if n >= len(widths):
                 return
             if n == 0:
-                scaled[item] = work.tile([P, len(widths), PAIR, HALF], F32, name="scaled")
-                low[item] = small.tile([P, 2], F32, name="low")
+                scaled[unit, grp] = work.tile([P, len(widths), PAIR, HALF], F32, name="scaled")
+                low[unit, grp] = small.tile([P, 2], F32, name="low")
             nc.vector.tensor_scalar(
-                out=scaled[item][:, n, :, 0 : widths[n]],
-                in0=banks[item][n][:, :, 0 : widths[n]],
+                out=scaled[unit, grp][:, n, :, 0 : widths[n]],
+                in0=banks[unit, grp][n][:, :, 0 : widths[n]],
                 scalar1=-SCALE,
-                scalar2=(None if n == 0 else low[item][:, n - 1 : n]),
+                scalar2=(None if n == 0 else low[unit, grp][:, n - 1 : n]),
                 op0=ALU.mult,
                 op1=ALU.min,
-                accum_out=low[item][:, n : n + 1],
+                accum_out=low[unit, grp][:, n : n + 1],
             )
 
-        def exponential(item):
-            i, h, grp = tile_head_group(item)
-            unit = item // N_GROUPS
-            n_pass = passes_of(item)
-            if grp == 0:
+        def exponential(unit, grp):
+            n_pass = passes_of(unit)
+            if unit not in sums:
                 sums[unit] = small.tile([P, N_GROUPS, n_pass], F32, name="sums")
-            e_of[item] = e_bufs[item % N_E_BUFS]
-            for g, width in enumerate(widths_of(item)):
+            e_of[unit, grp] = e_bufs[N_GROUPS * (unit % 2) + grp]
+            for g, width in enumerate(widths_of(unit)):
                 nc.scalar.activation(
-                    out=e_of[item][:, g, :, 0:width],
-                    in_=scaled[item][:, g, :, 0:width],
+                    out=e_of[unit, grp][:, g, :, 0:width],
+                    in_=scaled[unit, grp][:, g, :, 0:width],
                     func=ACT.Exp,
-                    bias=low[item][:, n_pass - 1 : n_pass],
+                    bias=low[unit, grp][:, n_pass - 1 : n_pass],
                     scale=-1.0,
                     accum_out=sums[unit][:, grp, g : g + 1],
                 )
 
-        def transpose_e(item):
-            n_pass = passes_of(item)
-            planes[item] = psum_t.tile([P, n_pass, PAIR, P], F32, tag="t", name="planes")
-            e_buf = e_of.pop(item)
+        def transpose_e(unit, grp):
+            n_pass = passes_of(unit)
+            if n_pass == 1:
+                if unit not in planes:
+                    planes[unit] = psum_t.tile([P, N_GROUPS, PAIR, P], F32, tag="t", name="planes")
+                bank = planes[unit][:, grp]
+                outs = [bank]
+            else:
+                planes[unit, grp] = psum_t.tile([P, n_pass, PAIR, P], F32, tag="t", name="planes")
+                outs = [planes[unit, grp][:, g] for g in range(n_pass)]
+            e_buf = e_of.pop((unit, grp))
             for g in range(n_pass):
                 for u in range(PAIR):
-                    nc.tensor.transpose(
-                        planes[item][:, g, u, :], e_buf[:, g, u, :].bitcast(F32), ident_f32[:]
+                    nc.tensor.transpose(outs[g][:, u, :], e_buf[:, g, u, :].bitcast(F32), ident_f32[:])
+
+        def group_e(unit, grp):
+            n_pass = passes_of(unit)
+            if unit not in e_grouped:
+                e_grouped[unit] = work.tile(
+                    [P, N_GROUPS, n_pass, P, PAIR], F32, name="e_grouped", align_bytes=64
+                )
+            if n_pass == 1:
+                if grp == 1:
+                    nc.scalar.copy(
+                        out=e_grouped[unit][:, :, 0], in_=planes[unit][:].rearrange("p a u q -> p a q u")
                     )
+            else:
+                nc.scalar.copy(
+                    out=e_grouped[unit][:, grp], in_=planes[unit, grp][:].rearrange("p g u q -> p g q u")
+                )
 
-        def group_e(item):
-            n_pass = passes_of(item)
-            e_grouped[item] = work.tile([P, n_pass, P, PAIR], F32, name="e_grouped", align_bytes=64)
-            nc.scalar.copy(out=e_grouped[item][:], in_=planes[item][:].rearrange("p g u q -> p g q u"))
-
-        def quantise_e(item):
-            width = passes_of(item) * P
-            e_codes[item] = work.tile([P, width], U32, name="e_codes", align_bytes=64)
-            e_scales[item] = work.tile([P, width], U8, name="e_scales", align_bytes=64)
+        def quantise_e(unit):
+            width = N_GROUPS * passes_of(unit) * P
+            e_codes[unit] = work.tile([P, width], U32, name="e_codes", align_bytes=64)
+            e_scales[unit] = work.tile([P, width], U8, name="e_scales", align_bytes=64)
             nc.vector.quantize_mx(
-                out=e_codes[item][:].bitcast(FP8X4),
-                scales=e_scales[item][:],
-                in_=e_grouped[item][:].rearrange("p g q u -> p (g q u)").bitcast(BF16),
+                out=e_codes[unit][:].bitcast(FP8X4),
+                scales=e_scales[unit][:],
+                in_=e_grouped[unit][:].rearrange("p a g q u -> p (a g q u)").bitcast(BF16),
             )
 
-        def attend(item):
-            i, h, grp = tile_head_group(item)
-            n_pass = passes_of(item)
-            acc[item] = psum_y.tile([P, V_WIDTH], F32, tag="y", name="acc")
+        def attend(unit, grp):
+            h = unit % N_VHEADS
+            n_pass = passes_of(unit)
+            acc[unit, grp] = psum_y.tile([P, V_WIDTH], F32, tag="y", name="acc")
             for g in range(n_pass):
-                cols = slice(g * P, (g + 1) * P)
+                cols = slice((grp * n_pass + g) * P, (grp * n_pass + g + 1) * P)
                 nc.tensor.matmul_mx(
-                    out=acc[item][:],
-                    lhsT=e_codes[item][:, cols].bitcast(FP8X4),
-                    lhsT_scale=e_scales[item][:, cols],
+                    out=acc[unit, grp][:],
+                    lhsT=e_codes[unit][:, cols].bitcast(FP8X4),
+                    lhsT_scale=e_scales[unit][:, cols],
                     rhs=v_codes[:, g, h, :].bitcast(FP8X4),
                     rhs_scale=v_scales[:, g, h, :],
                     start=(g == 0),
@@ -327,7 +336,7 @@ def tile_mixerdiffattention_pb_kernel(
 
         def compute_factors(unit):
             inverse[unit] = small.tile([P, N_GROUPS], F32, name="inverse")
-            if passes_of(N_GROUPS * unit) == 1:
+            if passes_of(unit) == 1:
                 total = sums[unit][:, :, 0]
             else:
                 both = small.tile([P, N_GROUPS], F32, name="both")
@@ -341,73 +350,85 @@ def tile_mixerdiffattention_pb_kernel(
                 out=factor[unit][:], in0=inverse[unit][:, 1:2], in1=minus_lam[:], op=ALU.mult
             )
 
-        def combine(item):
-            i, h, grp = tile_head_group(item)
-            unit = item // N_GROUPS
-            if grp == 0:
-                first[unit] = work.tile([P, V_WIDTH], F32, name="first")
-                nc.scalar.activation(
-                    out=first[unit][:], in_=acc[item][:], func=ACT.Copy, scale=inverse[unit][:, 0:1]
-                )
-            else:
-                result = work.tile([P, V_WIDTH], F32, name="result")
-                nc.vector.scalar_tensor_tensor(
-                    out=result[:],
-                    in0=acc[item][:],
-                    scalar=factor[unit][:],
-                    in1=first[unit][:],
-                    op0=ALU.mult,
-                    op1=ALU.add,
-                )
-                nc.sync.dma_start(
-                    out=out_tiles[i][:, h * V_WIDTH : (h + 1) * V_WIDTH], in_=result[:]
-                )
+        def scale_first_group(unit):
+            first[unit] = work.tile([P, V_WIDTH], F32, name="first")
+            nc.scalar.activation(
+                out=first[unit][:], in_=acc[unit, 0][:], func=ACT.Copy, scale=inverse[unit][:, 0:1]
+            )
+
+        def add_second_group_and_store(unit):
+            i, h = unit // N_VHEADS, unit % N_VHEADS
+            result = work.tile([P, V_WIDTH], F32, name="result")
+            nc.vector.scalar_tensor_tensor(
+                out=result[:],
+                in0=acc[unit, 1][:],
+                scalar=factor[unit][:],
+                in1=first[unit][:],
+                op0=ALU.mult,
+                op1=ALU.add,
+            )
+            nc.sync.dma_start(
+                out=out_tiles[i][:, h * V_WIDTH : (h + 1) * V_WIDTH], in_=result[:]
+            )
 
         ctx.enter_context(tc.manual_schedule())
         transpose_q_and_k(0, 0)
         transpose_q_and_k(0, 1)
-        group_v(0, 0, True)
-        group_v(0, 1, True)
-        quantise_v(0, 0)
         load_q_and_k(4)
 
-        def live(item):
-            return 0 <= item < N_ITEMS
+        def live(unit):
+            return 0 <= unit < N_UNITS
 
-        for step in range(N_ITEMS + 7):
+        for step in range(N_UNITS + 3):
             if live(step):
-                score(step)
-                find_maximum(step, 0)
-            if live(step - 3):
-                quantise_e(step - 3)
+                score(step, 0)
+                find_maximum(step, 0, 0)
+            if live(step - 1):
+                exponential(step - 1, 1)
             if live(step):
-                find_maximum(step, 1)
+                score(step, 1)
+                find_maximum(step, 1, 0)
+                find_maximum(step, 0, 1)
+                find_maximum(step, 1, 1)
             if live(step - 2):
-                transpose_e(step - 2)
-                group_e(step - 2)
-            if step == 3:
+                group_e(step - 2, 1)
+            if live(step - 3):
+                attend(step - 3, 0)
+                attend(step - 3, 1)
+                scale_first_group(step - 3)
+            if live(step - 2):
+                quantise_e(step - 2)
+            if live(step - 1):
+                transpose_e(step - 1, 0)
+            if live(step):
+                exponential(step, 0)
+            if live(step - 2):
+                compute_factors(step - 2)
+            if live(step - 1):
+                transpose_e(step - 1, 1)
+                group_e(step - 1, 0)
+            if live(step - 3):
+                add_second_group_and_store(step - 3)
+            if step == 0:
                 compute_lam()
-            if live(step - 3) and step % 2 == 0:
-                compute_factors((step - 3) // 2)
-            if step % 2 == 1 and step < 4 * (N_TILES - 1):
-                tile_ahead, half = 1 + step // 4, (step // 2) % 2
+                group_v(0, 2, False)
+                group_v(0, 0, True)
+                group_v(0, 3, False)
+            if step == 1:
+                quantise_v(0, 0)
+                group_v(0, 1, True)
+            if step == 2:
+                quantise_v(0, 1)
+            if step in (4, 5):
+                quantise_v(0, step - 2)
+            if 1 <= step <= N_VHEADS:
+                load_v(1, step - 1)
+            if step in (6, 8, 10, 12):
+                group_v(1, step // 2 - 3, False)
+            if step in (10, 12, 14, 16):
+                quantise_v(1, step // 2 - 5)
+            if step < 2 * (N_TILES - 1):
+                tile_ahead, half = 1 + step // 2, step % 2
                 transpose_q_and_k(tile_ahead, half)
                 if half == 1 and tile_ahead + 4 < N_TILES:
                     load_q_and_k(tile_ahead + 4)
-            if step < 2:
-                group_v(0, 2 + step, False)
-            if step in (2, 4, 6, 8):
-                load_v(1, step // 2 - 1)
-            if step == 2:
-                quantise_v(0, 1)
-            if step in (8, 10):
-                quantise_v(0, step // 2 - 2)
-            if 12 <= step < 28 and step % 4 == 0:
-                group_v(1, (step - 12) // 4, False)
-            if 20 <= step < 36 and step % 4 == 0:
-                quantise_v(1, (step - 20) // 4)
-            if live(step - 6):
-                attend(step - 6)
-                combine(step - 6)
-            if live(step):
-                exponential(step)

@@ -181,16 +181,25 @@ def tile_mixerdiffattention_pb_kernel(
         v_scales = keep.tile([P, 2, N_VHEADS, V_WIDTH], U8, name="v_scales", align_bytes=64)
         v_groups = {}
 
-        def group_v(g, h, on_vector):
-            v_groups[g, h] = work.tile([P, V_WIDTH, PACK], BF16, name="v_grouped", align_bytes=64)
-            out_ap = v_groups[g, h][:].rearrange("p (c n) j -> p c j n", n=4)
-            in_ap = v_raw[g, h][:].rearrange("p j (c n) -> p c j n", n=4)
+        def group_v(g, h, on_vector, quarters=range(4)):
+            if 0 in quarters:
+                v_groups[g, h] = work.tile([P, V_WIDTH, PACK], BF16, name="v_grouped", align_bytes=64)
+            groups = v_groups[g, h][:].rearrange("p (c n) j -> p c j n", n=4)
+            rows = v_raw[g, h][:].rearrange("p j (c n) -> p c j n", n=4)
             if on_vector:
-                nc.vector.tensor_copy(out=out_ap, in_=in_ap)
+                nc.vector.tensor_copy(out=groups, in_=rows)
             else:
-                nc.gpsimd.tensor_scalar(
-                    out=out_ap, in0=in_ap, scalar1=1.0, scalar2=0.0, op0=ALU.mult, op1=ALU.add
-                )
+                n_cols = V_WIDTH // 4 // 4
+                for part in quarters:
+                    cols = slice(part * n_cols, (part + 1) * n_cols)
+                    nc.gpsimd.tensor_scalar(
+                        out=groups[:, cols],
+                        in0=rows[:, cols],
+                        scalar1=1.0,
+                        scalar2=0.0,
+                        op0=ALU.mult,
+                        op1=ALU.add,
+                    )
 
         def quantise_v(g, h):
             nc.vector.quantize_mx(
@@ -304,7 +313,8 @@ def tile_mixerdiffattention_pb_kernel(
                         out=e_grouped[unit][:, :, 0], in_=planes[unit][:].rearrange("p a u q -> p a q u")
                     )
             else:
-                nc.scalar.copy(
+                copy = nc.vector.tensor_copy if grp == 0 and unit % 2 == 1 else nc.scalar.copy
+                copy(
                     out=e_grouped[unit][:, grp], in_=planes[unit, grp][:].rearrange("p g u q -> p g q u")
                 )
 
@@ -411,20 +421,20 @@ def tile_mixerdiffattention_pb_kernel(
                 add_second_group_and_store(step - 3)
             if step == 0:
                 compute_lam()
-                group_v(0, 2, False)
                 group_v(0, 0, True)
-                group_v(0, 3, False)
             if step == 1:
                 quantise_v(0, 0)
                 group_v(0, 1, True)
             if step == 2:
                 quantise_v(0, 1)
+            if step < 4:
+                group_v(0, 2 + step // 2, False, range(2 * (step % 2), 2 * (step % 2) + 2))
             if step in (4, 5):
                 quantise_v(0, step - 2)
             if 1 <= step <= N_VHEADS:
                 load_v(1, step - 1)
-            if step in (6, 8, 10, 12):
-                group_v(1, step // 2 - 3, False)
+            if 6 <= step < 14:
+                group_v(1, step // 2 - 3, False, range(2 * (step % 2), 2 * (step % 2) + 2))
             if step in (10, 12, 14, 16):
                 quantise_v(1, step // 2 - 5)
             if step < 2 * (N_TILES - 1):

@@ -35,7 +35,7 @@ N_UNITS = N_TILES * N_VHEADS
 N_ITEMS = N_UNITS * N_GROUPS
 
 FLOPS = N_HEADS * (512 * 512 + 512 * 1024) * 2 * (HEAD_DIM + V_WIDTH)
-N_E_BUFS = 4
+N_E_BUFS = 6
 
 def tile_mixerdiffattention_pb_kernel(
     tc, q_rot, k_rot, v, lambda_q1, lambda_k1, lambda_q2, lambda_k2, out
@@ -52,12 +52,24 @@ def tile_mixerdiffattention_pb_kernel(
 
         q_tiles = q_rot[0].rearrange("(i p) h d -> i p (h d)", p=P)
         k_tiles = k_rot[0].rearrange("(i p) h d -> i p (h d)", p=P)
+        q_halves = q_rot[0].rearrange("(i p) (a f n) d -> i f p a (n d)", p=P, a=N_GROUPS, f=2)
+        k_halves = k_rot[0].rearrange("(i p) (a f n) d -> i f p a (n d)", p=P, a=N_GROUPS, f=2)
         v_rows = v[0].rearrange("(g p j) h c -> g h p j c", p=P, j=PACK)
         out_tiles = out[0].rearrange("(i p) f -> i p f", p=P)
 
         q_raw = {}
         k_raw = {}
         v_raw = {}
+
+        def load_first_q_and_k():
+            q_raw[0] = raw.tile([P, N_HEADS * HEAD_DIM], BF16, name="q_raw")
+            k_raw[0] = raw.tile([P, N_HEADS * HEAD_DIM], BF16, name="k_raw")
+            for f in range(2):
+                for tile, halves in ((q_raw[0], q_halves), (k_raw[0], k_halves)):
+                    nc.sync.dma_start(
+                        out=tile[:].rearrange("p (a f w) -> p f a w", a=N_GROUPS, f=2)[:, f],
+                        in_=halves[0, f],
+                    )
 
         def load_q_and_k(i):
             q_raw[i] = raw.tile([P, N_HEADS * HEAD_DIM], BF16, name="q_raw")
@@ -75,7 +87,7 @@ def tile_mixerdiffattention_pb_kernel(
             nc.scalar.dma_start(out=lam_q[n : n + 1, :], in_=vec_q.unsqueeze(0))
             nc.scalar.dma_start(out=lam_k[n : n + 1, :], in_=vec_k.unsqueeze(0))
 
-        load_q_and_k(0)
+        load_first_q_and_k()
         load_v(0, 0)
         load_q_and_k(1)
         load_v(0, 1)
@@ -109,25 +121,26 @@ def tile_mixerdiffattention_pb_kernel(
             out=mask[:].rearrange("p u (r e) -> p u r e", e=PAIR),
             in_=mask_f32[:].rearrange("p (r u e) -> p u r e", u=PAIR, e=PAIR),
         )
-        e_bufs = []
-        for n in range(N_E_BUFS):
-            e_buf = keep.tile([P, 2, PAIR, HALF], BF16, name="e_buf%d" % n)
-            nc.gpsimd.memset(e_buf[:].bitcast(I32), 0)
-            e_bufs.append(e_buf)
-
         ones = keep.tile([P, P], F32, name="ones")
         nc.gpsimd.memset(ones[:], 1.0)
         lam_dot = keep.tile([P, 1], F32, name="lam_dot")
         nc.gpsimd.memset(lam_dot[:], 0.0)
+        e_bufs = []
+        for n in range(N_E_BUFS):
+            e_buf = keep.tile([P, PAIR, 2 * HALF], BF16, name="e_buf%d" % n)
+            nc.gpsimd.memset(e_buf[:].bitcast(I32), 0)
+            e_bufs.append(e_buf)
+
         minus_lam = keep.tile([P, 1], F32, name="minus_lam")
 
-        def compute_lam():
+        lam_diag = keep.tile([P, N_GROUPS], F32, name="lam_diag")
+
+        def compute_lam_dots():
             lam_prod = keep.tile([N_GROUPS, P], F32, name="lam_prod")
             nc.vector.tensor_tensor(out=lam_prod[:], in0=lam_q[:], in1=lam_k[:], op=ALU.mult)
             nc.vector.tensor_reduce(
                 out=lam_dot[0:N_GROUPS, :], in_=lam_prod[:], axis=AXIS.X, op=ALU.add
             )
-            lam_diag = keep.tile([P, N_GROUPS], F32, name="lam_diag")
             nc.vector.tensor_scalar(
                 out=lam_diag[:],
                 in0=ident_f32[:, 0:N_GROUPS],
@@ -135,6 +148,8 @@ def tile_mixerdiffattention_pb_kernel(
                 scalar2=None,
                 op0=ALU.mult,
             )
+
+        def compute_lam():
             lam_sum = psum_t.tile([P, N_GROUPS], F32, tag="t", name="lam_sum")
             nc.tensor.matmul(out=lam_sum[:], lhsT=ones[:], rhs=lam_diag[:], start=True, stop=True)
             lam_exp = keep.tile([P, N_GROUPS], F32, name="lam_exp")
@@ -175,7 +190,10 @@ def tile_mixerdiffattention_pb_kernel(
             g, column = i // TILES_PER_PASS, RUN * (i % TILES_PER_PASS)
             k_out = k_words[:, half, :, g, :, column : column + RUN]
             k_in = k_bank[:].rearrange("w a n (u x) -> w (a n) u x", u=PAIR)
-            nc.vector.tensor_copy(out=k_out, in_=k_in)
+            if half == 1 and i % 2 == 1:
+                nc.scalar.copy(out=k_out, in_=k_in)
+            else:
+                nc.vector.tensor_copy(out=k_out, in_=k_in)
 
         v_codes = keep.tile([P, 2, N_VHEADS, V_WIDTH], U32, name="v_codes", align_bytes=64)
         v_scales = keep.tile([P, 2, N_VHEADS, V_WIDTH], U8, name="v_scales", align_bytes=64)
@@ -208,8 +226,11 @@ def tile_mixerdiffattention_pb_kernel(
                 in_=v_groups[g, h][:].rearrange("p c j -> p (c j)"),
             )
 
+        units = [(i, h) for i in range(N_TILES) for h in range(N_VHEADS)]
+        units.append(units.pop(N_VHEADS - 1))
+
         def passes_of(unit):
-            return (unit // N_VHEADS) // TILES_PER_PASS + 1
+            return units[unit][0] // TILES_PER_PASS + 1
 
         banks = {}
         scaled = {}
@@ -226,11 +247,11 @@ def tile_mixerdiffattention_pb_kernel(
         first = {}
 
         def widths_of(unit):
-            i = unit // N_VHEADS
+            i = units[unit][0]
             return [HALF] * (i // TILES_PER_PASS) + [RUN * (i % TILES_PER_PASS + 1)]
 
         def score(unit, grp):
-            i, h = unit // N_VHEADS, unit % N_VHEADS
+            i, h = units[unit]
             widths = widths_of(unit)
             banks[unit, grp] = []
             for g, width in enumerate(widths):
@@ -259,10 +280,10 @@ def tile_mixerdiffattention_pb_kernel(
             if n >= len(widths):
                 return
             if n == 0:
-                scaled[unit, grp] = work.tile([P, len(widths), PAIR, HALF], F32, name="scaled")
+                scaled[unit, grp] = work.tile([P, PAIR, len(widths) * HALF], F32, name="scaled")
                 low[unit, grp] = small.tile([P, 2], F32, name="low")
             nc.vector.tensor_scalar(
-                out=scaled[unit, grp][:, n, :, 0 : widths[n]],
+                out=scaled[unit, grp][:, :, n * HALF : n * HALF + widths[n]],
                 in0=banks[unit, grp][n][:, :, 0 : widths[n]],
                 scalar1=-SCALE,
                 scalar2=(None if n == 0 else low[unit, grp][:, n - 1 : n]),
@@ -274,17 +295,18 @@ def tile_mixerdiffattention_pb_kernel(
         def exponential(unit, grp):
             n_pass = passes_of(unit)
             if unit not in sums:
-                sums[unit] = small.tile([P, N_GROUPS, n_pass], F32, name="sums")
-            e_of[unit, grp] = e_bufs[N_GROUPS * (unit % 2) + grp]
-            for g, width in enumerate(widths_of(unit)):
-                nc.scalar.activation(
-                    out=e_of[unit, grp][:, g, :, 0:width],
-                    in_=scaled[unit, grp][:, g, :, 0:width],
-                    func=ACT.Exp,
-                    bias=low[unit, grp][:, n_pass - 1 : n_pass],
-                    scale=-1.0,
-                    accum_out=sums[unit][:, grp, g : g + 1],
-                )
+                sums[unit] = small.tile([P, N_GROUPS], F32, name="sums")
+            turn = 2 if unit == N_UNITS - 1 else unit % 2
+            e_of[unit, grp] = e_bufs[N_GROUPS * turn + grp]
+            width = sum(widths_of(unit))
+            nc.scalar.activation(
+                out=e_of[unit, grp][:, :, 0:width],
+                in_=scaled[unit, grp][:, :, 0:width],
+                func=ACT.Exp,
+                bias=low[unit, grp][:, n_pass - 1 : n_pass],
+                scale=-1.0,
+                accum_out=sums[unit][:, grp : grp + 1],
+            )
 
         def transpose_e(unit, grp):
             n_pass = passes_of(unit)
@@ -299,7 +321,11 @@ def tile_mixerdiffattention_pb_kernel(
             e_buf = e_of.pop((unit, grp))
             for g in range(n_pass):
                 for u in range(PAIR):
-                    nc.tensor.transpose(outs[g][:, u, :], e_buf[:, g, u, :].bitcast(F32), ident_f32[:])
+                    nc.tensor.transpose(
+                        outs[g][:, u, :],
+                        e_buf[:, u, g * HALF : (g + 1) * HALF].bitcast(F32),
+                        ident_f32[:],
+                    )
 
         def group_e(unit, grp):
             n_pass = passes_of(unit)
@@ -329,7 +355,7 @@ def tile_mixerdiffattention_pb_kernel(
             )
 
         def attend(unit, grp):
-            h = unit % N_VHEADS
+            h = units[unit][1]
             n_pass = passes_of(unit)
             acc[unit, grp] = psum_y.tile([P, V_WIDTH], F32, tag="y", name="acc")
             for g in range(n_pass):
@@ -346,15 +372,7 @@ def tile_mixerdiffattention_pb_kernel(
 
         def compute_factors(unit):
             inverse[unit] = small.tile([P, N_GROUPS], F32, name="inverse")
-            if passes_of(unit) == 1:
-                total = sums[unit][:, :, 0]
-            else:
-                both = small.tile([P, N_GROUPS], F32, name="both")
-                nc.gpsimd.tensor_tensor(
-                    out=both[:], in0=sums[unit][:, :, 0], in1=sums[unit][:, :, 1], op=ALU.add
-                )
-                total = both[:]
-            nc.vector.reciprocal(out=inverse[unit][:], in_=total)
+            nc.vector.reciprocal(out=inverse[unit][:], in_=sums[unit][:])
             factor[unit] = small.tile([P, 1], F32, name="factor")
             nc.gpsimd.tensor_tensor(
                 out=factor[unit][:], in0=inverse[unit][:, 1:2], in1=minus_lam[:], op=ALU.mult
@@ -367,7 +385,7 @@ def tile_mixerdiffattention_pb_kernel(
             )
 
         def add_second_group_and_store(unit):
-            i, h = unit // N_VHEADS, unit % N_VHEADS
+            i, h = units[unit]
             result = work.tile([P, V_WIDTH], F32, name="result")
             nc.vector.scalar_tensor_tensor(
                 out=result[:],
@@ -420,9 +438,10 @@ def tile_mixerdiffattention_pb_kernel(
             if live(step - 3):
                 add_second_group_and_store(step - 3)
             if step == 0:
-                compute_lam()
+                compute_lam_dots()
                 group_v(0, 0, True)
             if step == 1:
+                compute_lam()
                 quantise_v(0, 0)
                 group_v(0, 1, True)
             if step == 2:

@@ -35,7 +35,7 @@ N_UNITS = N_TILES * N_VHEADS
 N_ITEMS = N_UNITS * N_GROUPS
 
 FLOPS = N_HEADS * (512 * 512 + 512 * 1024) * 2 * (HEAD_DIM + V_WIDTH)
-N_E_BUFS = 6
+N_E_BUFS = 10
 
 def tile_mixerdiffattention_pb_kernel(
     tc, q_rot, k_rot, v, lambda_q1, lambda_k1, lambda_q2, lambda_k2, out
@@ -127,9 +127,13 @@ def tile_mixerdiffattention_pb_kernel(
         nc.gpsimd.memset(lam_dot[:], 0.0)
         e_bufs = []
         for n in range(N_E_BUFS):
-            e_buf = keep.tile([P, PAIR, 2 * HALF], BF16, name="e_buf%d" % n)
-            nc.gpsimd.memset(e_buf[:].bitcast(I32), 0)
-            e_bufs.append(e_buf)
+            e_bufs.append(keep.tile([P, PAIR, 2 * HALF], BF16, name="e_buf%d" % n))
+
+        def zero_e_bufs(numbers):
+            for n in numbers:
+                nc.gpsimd.memset(e_bufs[n][:].bitcast(I32), 0)
+
+        zero_e_bufs(range(6))
 
         minus_lam = keep.tile([P, 1], F32, name="minus_lam")
 
@@ -226,7 +230,7 @@ def tile_mixerdiffattention_pb_kernel(
                 in_=v_groups[g, h][:].rearrange("p c j -> p (c j)"),
             )
 
-        units = [(i, h) for i in range(N_TILES) for h in range(N_VHEADS)]
+        units = [(i, h) for i in (0, 1, 2, 3, 5, 6, 7, 4) for h in range(N_VHEADS)]
         units.append(units.pop(N_VHEADS - 1))
 
         def passes_of(unit):
@@ -296,7 +300,12 @@ def tile_mixerdiffattention_pb_kernel(
             n_pass = passes_of(unit)
             if unit not in sums:
                 sums[unit] = small.tile([P, N_GROUPS], F32, name="sums")
-            turn = 2 if unit == N_UNITS - 1 else unit % 2
+            if unit == N_UNITS - 1:
+                turn = 2
+            elif units[unit][0] == TILES_PER_PASS:
+                turn = 3 + unit % 2
+            else:
+                turn = unit % 2
             e_of[unit, grp] = e_bufs[N_GROUPS * turn + grp]
             width = sum(widths_of(unit))
             nc.scalar.activation(
@@ -439,25 +448,32 @@ def tile_mixerdiffattention_pb_kernel(
                 add_second_group_and_store(step - 3)
             if step == 0:
                 compute_lam_dots()
-                group_v(0, 0, True)
             if step == 1:
+                group_v(0, 0, True)
                 compute_lam()
+            if step == 2:
                 quantise_v(0, 0)
                 group_v(0, 1, True)
-            if step == 2:
+            if step == 3:
                 quantise_v(0, 1)
             if step < 4:
-                group_v(0, 2 + step // 2, False, range(2 * (step % 2), 2 * (step % 2) + 2))
+                group_v(0, 2, False, (step,))
             if step in (4, 5):
-                quantise_v(0, step - 2)
-            if 1 <= step <= N_VHEADS:
-                load_v(1, step - 1)
+                group_v(0, 3, False, range(2 * (step % 2), 2 * (step % 2) + 2))
+            if step == 4:
+                quantise_v(0, 2)
+            if step == 7:
+                quantise_v(0, 3)
+            if step in (1, 2, 3, 5):
+                load_v(1, min(step, N_VHEADS) - 1)
             if 6 <= step < 14:
                 group_v(1, step // 2 - 3, False, range(2 * (step % 2), 2 * (step % 2) + 2))
+            if step == 14:
+                zero_e_bufs(range(6, N_E_BUFS))
             if step in (10, 12, 14, 16):
                 quantise_v(1, step // 2 - 5)
-            if step < 2 * (N_TILES - 1):
-                tile_ahead, half = 1 + step // 2, step % 2
+            if 1 <= step <= 2 * (N_TILES - 1):
+                tile_ahead, half = (step + 1) // 2, (step + 1) % 2
                 transpose_q_and_k(tile_ahead, half)
                 if half == 1 and tile_ahead + 4 < N_TILES:
                     load_q_and_k(tile_ahead + 4)

import math
from contextlib import ExitStack

import concourse.mybir as mybir
from concourse.masks import make_identity

F32 = mybir.dt.float32
BF16 = mybir.dt.bfloat16
I32 = mybir.dt.int32
U32 = mybir.dt.uint32
U8 = mybir.dt.uint8
FP8X4 = mybir.dt.float8_e4m3fn_x4
ALU = mybir.AluOpType
ACT = mybir.ActivationFunctionType
AXIS = mybir.AxisListType

P = 128
PAIR = 2
HALF = 256
RUN = 64
PACK = 4
K_PASS = P * PACK
SEQ = 1024
N_TILES = SEQ // P
TILES_PER_PASS = K_PASS // P
N_HEADS = 8
N_GROUPS = 2
N_VHEADS = 4
HEAD_DIM = 256
V_WIDTH = 512
SCALE = 1.0 / math.sqrt(HEAD_DIM)
LAMBDA_INIT = 0.8 - 0.6 * math.exp(-0.3 * 0)
MASKED = -1.0e30
N_UNITS = N_TILES * N_VHEADS
N_ITEMS = N_UNITS * N_GROUPS

FLOPS = N_HEADS * (512 * 512 + 512 * 1024) * 2 * (HEAD_DIM + V_WIDTH)
N_E_BUFS = 10

def tile_mixerdiffattention_pb_kernel(
    tc, q_rot, k_rot, v, lambda_q1, lambda_k1, lambda_q2, lambda_k2, out
):
    nc = tc.nc
    with ExitStack() as ctx:
        keep = ctx.enter_context(tc.tile_pool(name="keep", bufs=1))
        raw = ctx.enter_context(tc.tile_pool(name="raw", bufs=4))
        work = ctx.enter_context(tc.tile_pool(name="work", bufs=4))
        small = ctx.enter_context(tc.tile_pool(name="small", bufs=8))
        psum_s = ctx.enter_context(tc.psum_pool(name="psum_s", bufs=4))
        psum_t = ctx.enter_context(tc.psum_pool(name="psum_t", bufs=2))
        psum_y = ctx.enter_context(tc.psum_pool(name="psum_y", bufs=2))

        q_tiles = q_rot[0].rearrange("(i p) h d -> i p (h d)", p=P)
        k_tiles = k_rot[0].rearrange("(i p) h d -> i p (h d)", p=P)
        q_halves = q_rot[0].rearrange("(i p) (a f n) d -> i f p a (n d)", p=P, a=N_GROUPS, f=2)
        k_halves = k_rot[0].rearrange("(i p) (a f n) d -> i f p a (n d)", p=P, a=N_GROUPS, f=2)
        v_rows = v[0].rearrange("(g p j) h c -> g h p j c", p=P, j=PACK)
        out_tiles = out[0].rearrange("(i p) f -> i p f", p=P)

        q_raw = {}
        k_raw = {}
        v_raw = {}

        def load_first_q_and_k():
            q_raw[0] = raw.tile([P, N_HEADS * HEAD_DIM], BF16, name="q_raw")
            k_raw[0] = raw.tile([P, N_HEADS * HEAD_DIM], BF16, name="k_raw")
            for f in range(2):
                for tile, halves in ((q_raw[0], q_halves), (k_raw[0], k_halves)):
                    nc.sync.dma_start(
                        out=tile[:].rearrange("p (a f w) -> p f a w", a=N_GROUPS, f=2)[:, f],
                        in_=halves[0, f],
                    )

        def load_q_and_k(i):
            q_raw[i] = raw.tile([P, N_HEADS * HEAD_DIM], BF16, name="q_raw")
            nc.sync.dma_start(out=q_raw[i][:], in_=q_tiles[i])
            k_raw[i] = raw.tile([P, N_HEADS * HEAD_DIM], BF16, name="k_raw")
            nc.sync.dma_start(out=k_raw[i][:], in_=k_tiles[i])

        def load_v(g, h):
            v_raw[g, h] = raw.tile([P, PACK, V_WIDTH], BF16, name="v_raw")
            nc.sync.dma_start(out=v_raw[g, h][:], in_=v_rows[g, h])

        lam_q = keep.tile([N_GROUPS, P], BF16, name="lam_q")
        lam_k = keep.tile([N_GROUPS, P], BF16, name="lam_k")
        for n, (vec_q, vec_k) in enumerate(((lambda_q1, lambda_k1), (lambda_q2, lambda_k2))):
            nc.scalar.dma_start(out=lam_q[n : n + 1, :], in_=vec_q.unsqueeze(0))
            nc.scalar.dma_start(out=lam_k[n : n + 1, :], in_=vec_k.unsqueeze(0))

        load_first_q_and_k()
        load_v(0, 0)
        load_q_and_k(1)
        load_v(0, 1)
        load_v(0, 2)
        load_q_and_k(2)
        load_v(0, 3)
        load_q_and_k(3)

        ident_f32 = keep.tile([P, P], F32, name="ident_f32")
        make_identity(nc, ident_f32[:])
        ident_bf16 = keep.tile([P, P], BF16, name="ident_bf16")
        make_identity(nc, ident_bf16[:])
        to_planes = keep.tile([P, P], F32, name="to_planes")
        nc.vector.tensor_copy(
            out=to_planes[:].rearrange("p (u r e) -> p u r e", u=PAIR, e=PAIR),
            in_=ident_f32[:].rearrange("p (r u e) -> p u r e", u=PAIR, e=PAIR),
        )
        mask_f32 = keep.tile([P, P], F32, name="mask_f32")
        nc.gpsimd.memset(mask_f32[:], 0.0)
        nc.gpsimd.affine_select(
            out=mask_f32[:],
            in_=mask_f32[:],
            compare_op=ALU.is_ge,
            fill=MASKED,
            base=0,
            pattern=[[-1, P]],
            channel_multiplier=1,
        )
        mask = keep.tile([P, PAIR, RUN], BF16, name="mask")
        nc.vector.tensor_copy(
            out=mask[:].rearrange("p u (r e) -> p u r e", e=PAIR),
            in_=mask_f32[:].rearrange("p (r u e) -> p u r e", u=PAIR, e=PAIR),
        )
        ones = keep.tile([P, P], F32, name="ones")
        nc.gpsimd.memset(ones[:], 1.0)
        lam_dot = keep.tile([P, 1], F32, name="lam_dot")
        nc.gpsimd.memset(lam_dot[:], 0.0)
        e_bufs = []
        for n in range(N_E_BUFS):
            e_bufs.append(keep.tile([P, PAIR, 2 * HALF], BF16, name="e_buf%d" % n))

        def zero_e_bufs(numbers):
            for n in numbers:
                nc.gpsimd.memset(e_bufs[n][:].bitcast(I32), 0)

        zero_e_bufs(range(6))

        minus_lam = keep.tile([P, 1], F32, name="minus_lam")

        lam_diag = keep.tile([P, N_GROUPS], F32, name="lam_diag")

        def compute_lam_dots():
            lam_prod = keep.tile([N_GROUPS, P], F32, name="lam_prod")
            nc.vector.tensor_tensor(out=lam_prod[:], in0=lam_q[:], in1=lam_k[:], op=ALU.mult)
            nc.vector.tensor_reduce(
                out=lam_dot[0:N_GROUPS, :], in_=lam_prod[:], axis=AXIS.X, op=ALU.add
            )
            nc.vector.tensor_scalar(
                out=lam_diag[:],
                in0=ident_f32[:, 0:N_GROUPS],
                scalar1=lam_dot[:],
                scalar2=None,
                op0=ALU.mult,
            )

        def compute_lam():
            lam_sum = psum_t.tile([P, N_GROUPS], F32, tag="t", name="lam_sum")
            nc.tensor.matmul(out=lam_sum[:], lhsT=ones[:], rhs=lam_diag[:], start=True, stop=True)
            lam_exp = keep.tile([P, N_GROUPS], F32, name="lam_exp")
            nc.scalar.activation(out=lam_exp[:], in_=lam_sum[:], func=ACT.Exp)
            nc.vector.tensor_scalar(
                out=minus_lam[:],
                in0=lam_exp[:, 1:2],
                scalar1=lam_exp[:, 0:1],
                scalar2=LAMBDA_INIT,
                op0=ALU.subtract,
                op1=ALU.subtract,
            )

        q_t = keep.tile([P, N_TILES, N_GROUPS, N_VHEADS, P], F32, name="q_t")
        k_t = keep.tile([P, 2, N_GROUPS, 2, SEQ], F32, name="k_t")
        q_pairs = q_t[:].bitcast(BF16).rearrange("w i a h (q e) -> w i a h q e", e=2)
        k_pairs = k_t[:].bitcast(BF16).rearrange(
            "w f a n (g u x e) -> w f a n g u x e", u=PAIR, x=HALF, e=2
        )
        k_words = k_t[:].rearrange("w f a n (g u x) -> w f (a n) g u x", u=PAIR, x=HALF)

        def transpose_q_and_k(i, half):
            q_bank = psum_s.tile([P, N_GROUPS, 2, P], F32, tag="s", name="q_bank")
            k_bank = psum_s.tile([P, N_GROUPS, 2, P], F32, tag="s", name="k_bank")
            for bank, source, order in (
                (q_bank, q_raw[i], ident_f32),
                (k_bank, k_raw[i], to_planes),
            ):
                for grp in range(N_GROUPS):
                    for n in range(2):
                        head = N_VHEADS * grp + 2 * half + n
                        words = slice(head * P, (head + 1) * P)
                        nc.tensor.transpose(
                            bank[:, grp, n, :], source[:].bitcast(F32)[:, words], order[:]
                        )
            pair = slice(2 * half, 2 * half + 2)
            nc.scalar.copy(out=q_t[:, i, :, pair, :], in_=q_bank[:])
            g, column = i // TILES_PER_PASS, RUN * (i % TILES_PER_PASS)
            k_out = k_words[:, half, :, g, :, column : column + RUN]
            k_in = k_bank[:].rearrange("w a n (u x) -> w (a n) u x", u=PAIR)
            if half == 1 and i % 2 == 1:
                nc.scalar.copy(out=k_out, in_=k_in)
            else:
                nc.vector.tensor_copy(out=k_out, in_=k_in)

        v_codes = keep.tile([P, 2, N_VHEADS, V_WIDTH], U32, name="v_codes", align_bytes=64)
        v_scales = keep.tile([P, 2, N_VHEADS, V_WIDTH], U8, name="v_scales", align_bytes=64)
        v_groups = {}

        def group_v(g, h, on_vector, quarters=range(4)):
            if 0 in quarters:
                v_groups[g, h] = work.tile([P, V_WIDTH, PACK], BF16, name="v_grouped", align_bytes=64)
            groups = v_groups[g, h][:].rearrange("p (c n) j -> p c j n", n=4)
            rows = v_raw[g, h][:].rearrange("p j (c n) -> p c j n", n=4)
            if on_vector:
                nc.vector.tensor_copy(out=groups, in_=rows)
            else:
                n_cols = V_WIDTH // 4 // 4
                for part in quarters:
                    cols = slice(part * n_cols, (part + 1) * n_cols)
                    nc.gpsimd.tensor_scalar(
                        out=groups[:, cols],
                        in0=rows[:, cols],
                        scalar1=1.0,
                        scalar2=0.0,
                        op0=ALU.mult,
                        op1=ALU.add,
                    )

        def quantise_v(g, h):
            nc.vector.quantize_mx(
                out=v_codes[:, g, h, :].bitcast(FP8X4),
                scales=v_scales[:, g, h, :],
                in_=v_groups[g, h][:].rearrange("p c j -> p (c j)"),
            )

        units = [(i, h) for i in (0, 1, 2, 3, 5, 6, 7, 4) for h in range(N_VHEADS)]
        units.append(units.pop(N_VHEADS - 1))

        def passes_of(unit):
            return units[unit][0] // TILES_PER_PASS + 1

        banks = {}
        scaled = {}
        low = {}
        e_of = {}
        sums = {}
        planes = {}
        e_grouped = {}
        e_codes = {}
        e_scales = {}
        acc = {}
        inverse = {}
        factor = {}
        first = {}

        def widths_of(unit):
            i = units[unit][0]
            return [HALF] * (i // TILES_PER_PASS) + [RUN * (i % TILES_PER_PASS + 1)]

        def score(unit, grp):
            i, h = units[unit]
            widths = widths_of(unit)
            banks[unit, grp] = []
            for g, width in enumerate(widths):
                last = g == len(widths) - 1
                s = psum_s.tile([P, PAIR, HALF], F32, tag="s", name="s")
                for parity in range(2):
                    nc.tensor.matmul(
                        out=s[:, :, 0:width],
                        lhsT=q_pairs[:, i, grp, h, :, parity],
                        rhs=k_pairs[:, h // 2, grp, h % 2, g, :, 0:width, parity],
                        start=(parity == 0),
                        stop=(parity == 1 and not last),
                    )
                if last:
                    nc.tensor.matmul(
                        out=s[:, :, width - RUN : width],
                        lhsT=ident_bf16[:],
                        rhs=mask[:],
                        start=False,
                        stop=True,
                    )
                banks[unit, grp].append(s)

        def find_maximum(unit, grp, n):
            widths = widths_of(unit)
            if n >= len(widths):
                return
            if n == 0:
                scaled[unit, grp] = work.tile([P, PAIR, len(widths) * HALF], F32, name="scaled")
                low[unit, grp] = small.tile([P, 2], F32, name="low")
            nc.vector.tensor_scalar(
                out=scaled[unit, grp][:, :, n * HALF : n * HALF + widths[n]],
                in0=banks[unit, grp][n][:, :, 0 : widths[n]],
                scalar1=-SCALE,
                scalar2=(None if n == 0 else low[unit, grp][:, n - 1 : n]),
                op0=ALU.mult,
                op1=ALU.min,
                accum_out=low[unit, grp][:, n : n + 1],
            )

        def exponential(unit, grp):
            n_pass = passes_of(unit)
            if unit not in sums:
                sums[unit] = small.tile([P, N_GROUPS], F32, name="sums")
            if unit == N_UNITS - 1:
                turn = 2
            elif units[unit][0] == TILES_PER_PASS:
                turn = 3 + unit % 2
            else:
                turn = unit % 2
            e_of[unit, grp] = e_bufs[N_GROUPS * turn + grp]
            width = sum(widths_of(unit))
            nc.scalar.activation(
                out=e_of[unit, grp][:, :, 0:width],
                in_=scaled[unit, grp][:, :, 0:width],
                func=ACT.Exp,
                bias=low[unit, grp][:, n_pass - 1 : n_pass],
                scale=-1.0,
                accum_out=sums[unit][:, grp : grp + 1],
            )

        def transpose_e(unit, grp):
            n_pass = passes_of(unit)
            if n_pass == 1:
                if unit not in planes:
                    planes[unit] = psum_t.tile([P, N_GROUPS, PAIR, P], F32, tag="t", name="planes")
                bank = planes[unit][:, grp]
                outs = [bank]
            else:
                planes[unit, grp] = psum_t.tile([P, n_pass, PAIR, P], F32, tag="t", name="planes")
                outs = [planes[unit, grp][:, g] for g in range(n_pass)]
            e_buf = e_of.pop((unit, grp))
            for g in range(n_pass):
                for u in range(PAIR):
                    nc.tensor.transpose(
                        outs[g][:, u, :],
                        e_buf[:, u, g * HALF : (g + 1) * HALF].bitcast(F32),
                        ident_f32[:],
                    )

        def group_e(unit, grp):
            n_pass = passes_of(unit)
            if unit not in e_grouped:
                e_grouped[unit] = work.tile(
                    [P, N_GROUPS, n_pass, P, PAIR], F32, name="e_grouped", align_bytes=64
                )
            if n_pass == 1:
                if grp == 1:
                    nc.scalar.copy(
                        out=e_grouped[unit][:, :, 0], in_=planes[unit][:].rearrange("p a u q -> p a q u")
                    )
            else:
                copy = nc.vector.tensor_copy if grp == 0 and unit % 2 == 1 else nc.scalar.copy
                copy(
                    out=e_grouped[unit][:, grp], in_=planes[unit, grp][:].rearrange("p g u q -> p g q u")
                )

        def quantise_e(unit):
            width = N_GROUPS * passes_of(unit) * P
            e_codes[unit] = work.tile([P, width], U32, name="e_codes", align_bytes=64)
            e_scales[unit] = work.tile([P, width], U8, name="e_scales", align_bytes=64)
            nc.vector.quantize_mx(
                out=e_codes[unit][:].bitcast(FP8X4),
                scales=e_scales[unit][:],
                in_=e_grouped[unit][:].rearrange("p a g q u -> p (a g q u)").bitcast(BF16),
            )

        def attend(unit, grp):
            h = units[unit][1]
            n_pass = passes_of(unit)
            acc[unit, grp] = psum_y.tile([P, V_WIDTH], F32, tag="y", name="acc")
            for g in range(n_pass):
                cols = slice((grp * n_pass + g) * P, (grp * n_pass + g + 1) * P)
                nc.tensor.matmul_mx(
                    out=acc[unit, grp][:],
                    lhsT=e_codes[unit][:, cols].bitcast(FP8X4),
                    lhsT_scale=e_scales[unit][:, cols],
                    rhs=v_codes[:, g, h, :].bitcast(FP8X4),
                    rhs_scale=v_scales[:, g, h, :],
                    start=(g == 0),
                    stop=(g == n_pass - 1),
                )

        def compute_factors(unit):
            inverse[unit] = small.tile([P, N_GROUPS], F32, name="inverse")
            nc.vector.reciprocal(out=inverse[unit][:], in_=sums[unit][:])
            factor[unit] = small.tile([P, 1], F32, name="factor")
            nc.gpsimd.tensor_tensor(
                out=factor[unit][:], in0=inverse[unit][:, 1:2], in1=minus_lam[:], op=ALU.mult
            )

        def scale_first_group(unit):
            first[unit] = work.tile([P, V_WIDTH], F32, name="first")
            nc.scalar.activation(
                out=first[unit][:], in_=acc[unit, 0][:], func=ACT.Copy, scale=inverse[unit][:, 0:1]
            )

        def add_second_group_and_store(unit):
            i, h = units[unit]
            result = work.tile([P, V_WIDTH], F32, name="result")
            nc.vector.scalar_tensor_tensor(
                out=result[:],
                in0=acc[unit, 1][:],
                scalar=factor[unit][:],
                in1=first[unit][:],
                op0=ALU.mult,
                op1=ALU.add,
            )
            nc.sync.dma_start(
                out=out_tiles[i][:, h * V_WIDTH : (h + 1) * V_WIDTH], in_=result[:]
            )

        ctx.enter_context(tc.manual_schedule())
        transpose_q_and_k(0, 0)
        transpose_q_and_k(0, 1)
        load_q_and_k(4)

        def live(unit):
            return 0 <= unit < N_UNITS

        for step in range(N_UNITS + 3):
            if live(step):
                score(step, 0)
                find_maximum(step, 0, 0)
            if live(step - 1):
                exponential(step - 1, 1)
            if live(step):
                score(step, 1)
                find_maximum(step, 1, 0)
                find_maximum(step, 0, 1)
                find_maximum(step, 1, 1)
            if live(step - 2):
                group_e(step - 2, 1)
            if live(step - 3):
                attend(step - 3, 0)
                attend(step - 3, 1)
                scale_first_group(step - 3)
            if live(step - 2):
                quantise_e(step - 2)
            if live(step - 1):
                transpose_e(step - 1, 0)
            if live(step):
                exponential(step, 0)
            if live(step - 2):
                compute_factors(step - 2)
            if live(step - 1):
                transpose_e(step - 1, 1)
                group_e(step - 1, 0)
            if live(step - 3):
                add_second_group_and_store(step - 3)
            if step == 0:
                compute_lam_dots()
            if step == 1:
                group_v(0, 0, True)
                compute_lam()
            if step == 2:
                quantise_v(0, 0)
                group_v(0, 1, True)
            if step == 3:
                quantise_v(0, 1)
            if step < 4:
                group_v(0, 2, False, (step,))
            if step in (4, 5):
                group_v(0, 3, False, range(2 * (step % 2), 2 * (step % 2) + 2))
            if step == 4:
                quantise_v(0, 2)
            if step == 7:
                quantise_v(0, 3)
            if step in (1, 2, 3, 5):
                load_v(1, min(step, N_VHEADS) - 1)
            if 6 <= step < 14:
                group_v(1, step // 2 - 3, False, range(2 * (step % 2), 2 * (step % 2) + 2))
            if step == 14:
                zero_e_bufs(range(6, N_E_BUFS))
            if step in (10, 12, 14, 16):
                quantise_v(1, step // 2 - 5)
            if 1 <= step <= 2 * (N_TILES - 1):
                tile_ahead, half = (step + 1) // 2, (step + 1) % 2
                transpose_q_and_k(tile_ahead, half)
                if half == 1 and tile_ahead + 4 < N_TILES:
                    load_q_and_k(tile_ahead + 4)
